import numpy as np
import ml_dtypes


def mxq(x, axis, fmt="e4m3"):
    dtype, down = {"e4m3": (ml_dtypes.float8_e4m3fn, 7), "e5m2": (ml_dtypes.float8_e5m2, 14)}[fmt]
    v = np.moveaxis(np.asarray(x, np.float32).astype(ml_dtypes.bfloat16).astype(np.float64), axis, -1)
    blocks = v.reshape(v.shape[:-1] + (-1, 32))
    amax = np.abs(blocks).max(-1, keepdims=True)
    byte = np.maximum(np.where(amax > 0, np.frexp(amax)[1] - 1 + 127, 0) - down, 1)
    scale = np.exp2(byte - 127.0)
    codes = (blocks / scale).astype(np.float32).astype(dtype).astype(np.float64)
    return np.moveaxis((codes * scale).reshape(v.shape), -1, axis)


WIDE = False


def mx_kscale(k):
    if not WIDE:
        return np.ones(k)
    levels = np.array([10, -10, 5, -5, 0])
    a = np.random.permutation(np.resize(levels, k // 512 * 4)).reshape(k // 512, 4)
    idx = np.arange(k)
    return np.exp2(a[idx // 512, idx % 128 // 32])


BF16 = ml_dtypes.bfloat16


def bf(x):
    return np.asarray(x, np.float32).astype(BF16)


def f64(x):
    return np.asarray(x).astype(np.float64)


B, C, IC, H, W = 16, 256, 512, 16, 32
N = H * W


def setup_inputs():
    t = mx_kscale(IC)
    a = 1.2 * IC ** -0.25
    return {"theta": bf(np.random.standard_normal((B, IC, N)) * a),
            "phi": bf(np.random.standard_normal((B, IC, N)) * a),
            "g_proj": bf(np.random.standard_normal((B, IC, N)) * t[None, :, None]),
            "pos_embedding": bf(np.random.standard_normal((1, N, N))),
            "pos_embedding_decoder": bf((1.5 + 0.5 * np.random.standard_normal((1, IC, H, W))) * t[None, :, None, None]),
            "w_mask": bf(np.random.standard_normal((C, IC)) * 2.0 / np.sqrt(IC) / t[None, :]),
            "x": bf(np.random.standard_normal((B, C, H, W)))}


def reference(theta, phi, g_proj, pos_embedding, pos_embedding_decoder, w_mask, x):
    s = f64(theta).transpose(0, 2, 1) @ f64(phi) + f64(pos_embedding)
    e = np.exp(s - s.max(1, keepdims=True))
    attn = e / e.sum(1, keepdims=True)
    g = (f64(g_proj) + f64(pos_embedding_decoder).reshape(1, IC, N)).transpose(0, 2, 1)
    y = mxq(attn, 2, "e4m3") @ mxq(g, 1, "e4m3")
    m = mxq(f64(w_mask), 1, "e4m3") @ mxq(y.transpose(0, 2, 1), 1, "e4m3")
    return m.reshape(B, C, H, W) + f64(x)

@@ -1,0 +1,267 @@
+from contextlib import ExitStack
+
+import concourse.mybir as mybir
+from concourse.masks import make_identity
+
+F32 = mybir.dt.float32
+BF16 = mybir.dt.bfloat16
+U32 = mybir.dt.uint32
+U8 = mybir.dt.uint8
+FP8X4 = mybir.dt.float8_e4m3fn_x4
+ALU = mybir.AluOpType
+ACT = mybir.ActivationFunctionType
+AXIS = mybir.AxisListType
+
+MAPS = 16
+CH = 512
+POS = 512
+OUT_CH = 256
+P = 128
+PACK = 4
+CHUNKS = CH // P
+OUT_BLOCKS = OUT_CH // P
+POS_ON_TENSOR = 2
+AHEAD = 3
+
+FLOPS = 2 * MAPS * (2 * POS * POS * CH + OUT_CH * CH * POS)
+
+
+def tile_nonlocalblock_pa_t_kernel(
+    tc, theta, phi, g_proj, pos_embedding, pos_embedding_decoder, w_mask, x, out
+):
+    nc = tc.nc
+    with ExitStack() as ctx:
+        const = ctx.enter_context(tc.tile_pool(name="const", bufs=1))
+        loads = ctx.enter_context(tc.tile_pool(name="loads", bufs=3))
+        work = ctx.enter_context(tc.tile_pool(name="work", bufs=2))
+        psum_scores = ctx.enter_context(tc.psum_pool(name="psum_scores", bufs=AHEAD))
+        psum_flip = ctx.enter_context(tc.psum_pool(name="psum_flip", bufs=2))
+        psum_mx = ctx.enter_context(tc.psum_pool(name="psum_mx", bufs=3))
+
+        ident = const.tile([P, P], F32)
+        make_identity(nc, ident[:])
+        ident_bf = const.tile([P, P], BF16)
+        make_identity(nc, ident_bf[:])
+
+        theta_of, phi_of, gproj_of, x_of = {}, {}, {}, {}
+        scores_of = {}
+        g_of, attn_of, y_of = {}, {}, {}
+
+        def load_map(b):
+            phi_sb = loads.tile([P, CHUNKS, 2, P, 2], BF16)
+            nc.sync.dma_start(
+                out=phi_sb[:].rearrange("p k u q e -> p (k u q e)"),
+                in_=phi[b].rearrange("(p k) n -> p (k n)", k=CHUNKS),
+            )
+            theta_sb = loads.tile([P, CHUNKS, POS], BF16)
+            nc.sync.dma_start(out=theta_sb[:], in_=theta[b].rearrange("(p k) n -> p k n", k=CHUNKS))
+            gproj_sb = loads.tile([P, CHUNKS * POS], BF16)
+            nc.sync.dma_start(out=gproj_sb[:], in_=g_proj[b].rearrange("(p k) n -> p (k n)", k=CHUNKS))
+            x_sb = loads.tile([P, OUT_BLOCKS, POS], BF16, bufs=4)
+            nc.sync.dma_start(out=x_sb[:], in_=x[b].rearrange("(p a) h w -> p a (h w)", a=OUT_BLOCKS))
+            phi_of[b], theta_of[b], gproj_of[b], x_of[b] = phi_sb, theta_sb, gproj_sb, x_sb
+
+        def flip_half(src, half):
+            words = src[:].bitcast(F32)
+            bank = psum_flip.tile([P, 2, 2, P], F32, tag="flip")
+            for h in range(2):
+                for u in range(2):
+                    first = (2 * half + h) * (POS // 2) + u * P
+                    nc.tensor.transpose(bank[:, h, u, :], words[:, first : first + P], ident[:])
+            return bank
+
+        def unload_half(bank, dst, half):
+            dst_words = dst[:].bitcast(F32).rearrange("p (k c u) -> p k c u", k=CHUNKS, u=2)
+            nc.scalar.copy(out=dst_words[:, 2 * half : 2 * half + 2, :, :], in_=bank[:].rearrange("p h u c -> p h c u"))
+
+        pos_sb = const.tile([P, PACK, POS], BF16)
+        nc.sync.dma_start(out=pos_sb[:], in_=pos_embedding[0].rearrange("(a p) j -> p a j", p=P))
+        load_map(0)
+        dec_sb = const.tile([P, CHUNKS * POS], BF16)
+        nc.sync.dma_start(
+            out=dec_sb[:], in_=pos_embedding_decoder[0].rearrange("(p k) h w -> p (k h w)", k=CHUNKS)
+        )
+        w_sb = const.tile([P, OUT_BLOCKS * CH], BF16)
+        nc.sync.dma_start(out=w_sb[:], in_=w_mask.rearrange("(p a) c -> p (a c)", a=OUT_BLOCKS))
+        load_map(1)
+
+        pos_t = const.tile([P, PACK, POS], BF16)
+        pos_words = pos_sb[:].rearrange("p a j -> p (a j)").bitcast(F32)
+        for u in range(2):
+            bank = psum_scores.tile([P, PACK, P], F32, tag="scores")
+            for a in range(PACK):
+                first = a * (POS // 2) + u * P
+                nc.tensor.transpose(bank[:, a, :], pos_words[:, first : first + P], ident[:])
+            pairs = bank[:].rearrange("p a i -> p (a i)").bitcast(BF16)
+            nc.vector.tensor_copy(out=pos_t[:, 2 * u : 2 * u + 2, :], in_=pairs.rearrange("p (i e) -> p e i", e=2))
+
+        def pos_on_tensor(t):
+            return t % 2 == 1 and t // 2 < POS_ON_TENSOR
+
+        def scores_block(n):
+            b, t = divmod(n, PACK)
+            u, e = divmod(t, 2)
+            acc = psum_scores.tile([P, POS], F32, tag="scores")
+            for k in range(CHUNKS):
+                nc.tensor.matmul(
+                    out=acc[:],
+                    lhsT=phi_of[b][:, k, u, :, e],
+                    rhs=theta_of[b][:, k, :],
+                    start=(k == 0),
+                    stop=(k == CHUNKS - 1 and not pos_on_tensor(t)),
+                )
+            if pos_on_tensor(t):
+                nc.tensor.matmul(out=acc[:], lhsT=ident_bf[:], rhs=pos_t[:, t, :], start=False, stop=True)
+            scores_of[n] = acc
+
+        for n in range(AHEAD):
+            scores_block(n)
+
+        dec_t = const.tile([P, CHUNKS * P * PACK], BF16)
+        for half in range(2):
+            unload_half(flip_half(dec_sb, half), dec_t, half)
+
+        w_grouped = const.tile([P, OUT_CH * PACK], BF16, align_bytes=64)
+        w_codes = const.tile([P, OUT_CH], U32, align_bytes=64)
+        w_scales = const.tile([P, OUT_CH], U8, align_bytes=64)
+        w_words = w_sb[:].bitcast(F32)
+        bank = psum_flip.tile([P, OUT_BLOCKS, 2, P], F32, tag="flip")
+        for a in range(OUT_BLOCKS):
+            for u in range(2):
+                nc.tensor.transpose(
+                    bank[:, a, u, :], w_words[:, a * (CH // 2) + u : (a + 1) * (CH // 2) : 2], ident[:]
+                )
+        nc.scalar.copy(
+            out=w_grouped[:].bitcast(F32).rearrange("p (a r u) -> p a r u", a=OUT_BLOCKS, u=2),
+            in_=bank[:].rearrange("p a u r -> p a r u"),
+        )
+        nc.vector.quantize_mx(out=w_codes[:].bitcast(FP8X4), scales=w_scales[:], in_=w_grouped[:])
+
+        soft_of = {}
+
+        def softmax_block(b, t):
+            if t == 0:
+                shifted = work.tile([P, PACK, POS], F32)
+                expd = work.tile([P, PACK, POS], F32)
+                neg_max = work.tile([P, PACK], F32)
+                row_sum = work.tile([P, PACK], F32)
+                soft_of[b] = (shifted, expd, neg_max, row_sum)
+            shifted, expd, neg_max, row_sum = soft_of[b]
+            if pos_on_tensor(t):
+                with_pos = scores_of[PACK * b + t][:]
+            else:
+                with_pos = shifted[:, t, :]
+                nc.vector.tensor_tensor(out=with_pos, in0=scores_of[PACK * b + t][:], in1=pos_t[:, t, :], op=ALU.add)
+            nc.vector.tensor_reduce(out=neg_max[:, t : t + 1], in_=with_pos, axis=AXIS.X, op=ALU.max, negate=True)
+            nc.scalar.activation(
+                out=expd[:, t, :],
+                in_=with_pos,
+                func=ACT.Exp,
+                bias=neg_max[:, t : t + 1],
+                scale=1.0,
+                accum_out=row_sum[:, t : t + 1],
+            )
+
+        def normalise(b):
+            expd, row_sum = soft_of[b][1], soft_of[b][3]
+            inv_sum = work.tile([P, PACK], F32)
+            nc.vector.reciprocal(out=inv_sum[:], in_=row_sum[:])
+            attn_bf = work.tile([P, POS, PACK], BF16, align_bytes=64)
+            nc.vector.tensor_tensor(
+                out=attn_bf[:],
+                in0=expd[:].rearrange("p t i -> p i t"),
+                in1=inv_sum[:].unsqueeze(1).to_broadcast([P, POS, PACK]),
+                op=ALU.mult,
+            )
+            return attn_bf
+
+        def quantise(what, grouped):
+            codes = work.tile([P, POS], U32, align_bytes=64, name=what + "_codes", tag=what + "_codes")
+            scales = work.tile([P, POS], U8, align_bytes=64, name=what + "_scales", tag=what + "_scales")
+            nc.vector.quantize_mx(out=codes[:].bitcast(FP8X4), scales=scales[:], in_=grouped)
+            return codes, scales
+
+        def add_decoder(g_raw):
+            g_bf = work.tile([P, CH * PACK], BF16, align_bytes=64)
+            for k in range(CHUNKS):
+                part = slice(k * P * PACK, (k + 1) * P * PACK)
+                nc.gpsimd.tensor_tensor(out=g_bf[:, part], in0=g_raw[:, part], in1=dec_t[:, part], op=ALU.add)
+            return g_bf
+
+        def mix(b):
+            g_codes, g_scales = g_of[b]
+            a_codes, a_scales = attn_of[b]
+            y_bf = work.tile([P, POS, PACK], BF16, align_bytes=64)
+            for r in range(POS // P):
+                cols = slice(r * P, (r + 1) * P)
+                bank = psum_mx.tile([P, PACK, P], F32, tag="mx")
+                for t in range(PACK):
+                    group = slice(t * P, (t + 1) * P)
+                    nc.tensor.matmul_mx(
+                        out=bank[:, t, :],
+                        lhsT=g_codes[:, group].bitcast(FP8X4),
+                        lhsT_scale=g_scales[:, group],
+                        rhs=a_codes[:, cols].bitcast(FP8X4),
+                        rhs_scale=a_scales[:, cols],
+                        start=True,
+                        stop=True,
+                    )
+                nc.scalar.copy(out=y_bf[:, cols, :], in_=bank[:].rearrange("p t i -> p i t"))
+            return y_bf
+
+        def project(b):
+            y_codes, y_scales = y_of[b]
+            result = work.tile([P, OUT_BLOCKS, POS], F32)
+            for a in range(OUT_BLOCKS):
+                rows = slice(a * P, (a + 1) * P)
+                bank = psum_mx.tile([P, POS], F32, tag="mx")
+                nc.tensor.matmul_mx(
+                    out=bank[:],
+                    lhsT=w_codes[:, rows].bitcast(FP8X4),
+                    lhsT_scale=w_scales[:, rows],
+                    rhs=y_codes[:].bitcast(FP8X4),
+                    rhs_scale=y_scales[:],
+                    start=True,
+                    stop=True,
+                )
+                nc.scalar.copy(out=result[:, a, :], in_=bank[:])
+                nc.gpsimd.tensor_tensor(out=result[:, a, :], in0=result[:, a, :], in1=x_of[b][:, a, :], op=ALU.add)
+            nc.sync.dma_start(out=out[b].rearrange("(p a) h w -> p a (h w)", a=OUT_BLOCKS), in_=result[:])
+
+        def flip_g(b):
+            return [flip_half(gproj_of[b], half) for half in range(2)]
+
+        def unload_g(banks):
+            g_raw = work.tile([P, CH * PACK], BF16)
+            for half in range(2):
+                unload_half(banks[half], g_raw, half)
+            return g_raw
+
+        g_bf_of = {0: add_decoder(unload_g(flip_g(0)))}
+
+        for k in range(MAPS + 1):
+            if k + 2 < MAPS:
+                load_map(k + 2)
+            if k >= 1:
+                y_bf = mix(k - 1)
+            if k < MAPS:
+                banks = []
+                for t in range(PACK):
+                    softmax_block(k, t)
+                    if PACK * k + t + AHEAD < PACK * MAPS:
+                        scores_block(PACK * k + t + AHEAD)
+                    if t < 2 and k + 1 < MAPS:
+                        banks.append(flip_half(gproj_of[k + 1], t))
+                if k + 1 < MAPS:
+                    g_raw = unload_g(banks)
+                g_of[k] = quantise("g", g_bf_of[k][:])
+            if k >= 1:
+                y_of[k - 1] = quantise("y", y_bf[:].rearrange("p i t -> p (i t)"))
+            if k < MAPS:
+                attn_bf = normalise(k)
+            if k >= 1:
+                project(k - 1)
+            if k + 1 < MAPS:
+                g_bf_of[k + 1] = add_decoder(g_raw)
+            if k < MAPS:
+                attn_of[k] = quantise("attn", attn_bf[:].rearrange("p i t -> p (i t)"))

@@ -57,7 +57,7 @@ def tile_nonlocalblock_pa_t_kernel(
             nc.sync.dma_start(out=theta_sb[:], in_=theta[b].rearrange("(p k) n -> p k n", k=CHUNKS))
             gproj_sb = loads.tile([P, CHUNKS * POS], BF16)
             nc.sync.dma_start(out=gproj_sb[:], in_=g_proj[b].rearrange("(p k) n -> p (k n)", k=CHUNKS))
-            x_sb = loads.tile([P, OUT_BLOCKS, POS], BF16, bufs=4)
+            x_sb = loads.tile([P, OUT_BLOCKS, POS], BF16, bufs=5)
             nc.sync.dma_start(out=x_sb[:], in_=x[b].rearrange("(p a) h w -> p a (h w)", a=OUT_BLOCKS))
             phi_of[b], theta_of[b], gproj_of[b], x_of[b] = phi_sb, theta_sb, gproj_sb, x_sb
 
@@ -145,8 +145,9 @@ def tile_nonlocalblock_pa_t_kernel(
                 expd = work.tile([P, PACK, POS], F32)
                 neg_max = work.tile([P, PACK], F32)
                 row_sum = work.tile([P, PACK], F32)
-                soft_of[b] = (shifted, expd, neg_max, row_sum)
-            shifted, expd, neg_max, row_sum = soft_of[b]
+                inv_sum = work.tile([P, PACK], F32)
+                soft_of[b] = (shifted, expd, neg_max, row_sum, inv_sum)
+            shifted, expd, neg_max, row_sum = soft_of[b][:4]
             if pos_on_tensor(t):
                 with_pos = scores_of[PACK * b + t][:]
             else:
@@ -162,16 +163,22 @@ def tile_nonlocalblock_pa_t_kernel(
                 accum_out=row_sum[:, t : t + 1],
             )
 
-        def normalise(b):
-            expd, row_sum = soft_of[b][1], soft_of[b][3]
-            inv_sum = work.tile([P, PACK], F32)
-            nc.vector.reciprocal(out=inv_sum[:], in_=row_sum[:])
+        def invert_sums(b, first):
+            row_sum, inv_sum = soft_of[b][3], soft_of[b][4]
+            nc.vector.reciprocal(out=inv_sum[:, first : first + 2], in_=row_sum[:, first : first + 2])
+
+        def scale_rows(b):
+            expd, inv_sum = soft_of[b][1], soft_of[b][4]
+            attn_rows = work.tile([P, PACK, POS], BF16)
+            for t in range(PACK):
+                nc.scalar.activation(out=attn_rows[:, t, :], in_=expd[:, t, :], func=ACT.Copy, scale=inv_sum[:, t : t + 1])
+            return attn_rows
+
+        def regroup(attn_rows):
             attn_bf = work.tile([P, POS, PACK], BF16, align_bytes=64)
-            nc.vector.tensor_tensor(
-                out=attn_bf[:],
-                in0=expd[:].rearrange("p t i -> p i t"),
-                in1=inv_sum[:].unsqueeze(1).to_broadcast([P, POS, PACK]),
-                op=ALU.mult,
+            nc.vector.tensor_copy(
+                out=attn_bf[:].rearrange("p (c i) t -> p c t i", i=4),
+                in_=attn_rows[:].rearrange("p t (c i) -> p c t i", i=4),
             )
             return attn_bf
 
@@ -183,9 +190,7 @@ def tile_nonlocalblock_pa_t_kernel(
 
         def add_decoder(g_raw):
             g_bf = work.tile([P, CH * PACK], BF16, align_bytes=64)
-            for k in range(CHUNKS):
-                part = slice(k * P * PACK, (k + 1) * P * PACK)
-                nc.gpsimd.tensor_tensor(out=g_bf[:, part], in0=g_raw[:, part], in1=dec_t[:, part], op=ALU.add)
+            nc.vector.tensor_tensor(out=g_bf[:], in0=g_raw[:], in1=dec_t[:], op=ALU.add)
             return g_bf
 
         def mix(b):
@@ -224,12 +229,8 @@ def tile_nonlocalblock_pa_t_kernel(
                     start=True,
                     stop=True,
                 )
-                nc.scalar.copy(out=result[:, a, :], in_=bank[:])
-                nc.gpsimd.tensor_tensor(out=result[:, a, :], in0=result[:, a, :], in1=x_of[b][:, a, :], op=ALU.add)
+                nc.vector.tensor_tensor(out=result[:, a, :], in0=bank[:], in1=x_of[b][:, a, :], op=ALU.add)
             nc.sync.dma_start(out=out[b].rearrange("(p a) h w -> p a (h w)", a=OUT_BLOCKS), in_=result[:])
-
-        def flip_g(b):
-            return [flip_half(gproj_of[b], half) for half in range(2)]
 
         def unload_g(banks):
             g_raw = work.tile([P, CH * PACK], BF16)
@@ -237,31 +238,38 @@ def tile_nonlocalblock_pa_t_kernel(
                 unload_half(banks[half], g_raw, half)
             return g_raw
 
-        g_bf_of = {0: add_decoder(unload_g(flip_g(0)))}
+        def live(b):
+            return 0 <= b < MAPS
 
-        for k in range(MAPS + 1):
-            if k + 2 < MAPS:
+        g_raw_of = {0: unload_g([flip_half(gproj_of[0], half) for half in range(2)])}
+        y_bf_of = {}
+
+        for k in range(MAPS + 2):
+            if live(k + 2):
                 load_map(k + 2)
-            if k >= 1:
-                y_bf = mix(k - 1)
-            if k < MAPS:
-                banks = []
+            banks = []
+            if live(k):
                 for t in range(PACK):
                     softmax_block(k, t)
                     if PACK * k + t + AHEAD < PACK * MAPS:
                         scores_block(PACK * k + t + AHEAD)
-                    if t < 2 and k + 1 < MAPS:
+                    if t < 2 and live(k + 1):
                         banks.append(flip_half(gproj_of[k + 1], t))
-                if k + 1 < MAPS:
-                    g_raw = unload_g(banks)
-                g_of[k] = quantise("g", g_bf_of[k][:])
-            if k >= 1:
-                y_of[k - 1] = quantise("y", y_bf[:].rearrange("p i t -> p (i t)"))
-            if k < MAPS:
-                attn_bf = normalise(k)
-            if k >= 1:
-                project(k - 1)
-            if k + 1 < MAPS:
-                g_bf_of[k + 1] = add_decoder(g_raw)
-            if k < MAPS:
+                invert_sums(k, 0)
+            if live(k - 2):
+                y_of[k - 2] = quantise("y", y_bf_of[k - 2][:].rearrange("p i t -> p (i t)"))
+            if live(k):
+                g_bf = add_decoder(g_raw_of[k])
+                invert_sums(k, 2)
+                attn_rows = scale_rows(k)
+            if live(k - 2):
+                project(k - 2)
+            if live(k):
+                g_of[k] = quantise("g", g_bf[:])
+            if live(k - 1):
+                y_bf_of[k - 1] = mix(k - 1)
+            if live(k + 1):
+                g_raw_of[k + 1] = unload_g(banks)
+            if live(k):
+                attn_bf = regroup(attn_rows)
                 attn_of[k] = quantise("attn", attn_bf[:].rearrange("p i t -> p (i t)"))

@@ -67,12 +67,15 @@ def tile_nonlocalblock_pa_t_kernel(
             for h in range(2):
                 for u in range(2):
                     first = (2 * half + h) * (POS // 2) + u * P
-                    nc.tensor.transpose(bank[:, h, u, :], words[:, first : first + P], ident[:])
+                    nc.tensor.transpose(bank[:, u, h, :], words[:, first : first + P], ident[:])
             return bank
 
         def unload_half(bank, dst, half):
-            dst_words = dst[:].bitcast(F32).rearrange("p (k c u) -> p k c u", k=CHUNKS, u=2)
-            nc.scalar.copy(out=dst_words[:, 2 * half : 2 * half + 2, :, :], in_=bank[:].rearrange("p h u c -> p h c u"))
+            half_words = CH * PACK // 4
+            dst_words = dst[:].bitcast(F32)[:, half * half_words : (half + 1) * half_words]
+            nc.scalar.copy(
+                out=dst_words.rearrange("p (c u) -> p c u", u=2), in_=bank[:].rearrange("p u h c -> p (h c) u")
+            )
 
         pos_sb = const.tile([P, PACK, POS], BF16)
         nc.sync.dma_start(out=pos_sb[:], in_=pos_embedding[0].rearrange("(a p) j -> p a j", p=P))
@@ -188,10 +191,15 @@ def tile_nonlocalblock_pa_t_kernel(
             nc.vector.quantize_mx(out=codes[:].bitcast(FP8X4), scales=scales[:], in_=grouped)
             return codes, scales
 
-        def add_decoder(g_raw):
-            g_bf = work.tile([P, CH * PACK], BF16, align_bytes=64)
-            nc.vector.tensor_tensor(out=g_bf[:], in0=g_raw[:], in1=dec_t[:], op=ALU.add)
-            return g_bf
+        def add_decoder(bank, g_bf, half):
+            cols = slice(half * CH * PACK // 2, (half + 1) * CH * PACK // 2)
+            pairs = bank[:].rearrange("p u h c -> p (u h c)").bitcast(BF16)
+            nc.vector.tensor_tensor(
+                out=g_bf[:, cols].rearrange("p (c u e) -> p c u e", u=2, e=2),
+                in0=pairs.rearrange("p (u c e) -> p c u e", u=2, e=2),
+                in1=dec_t[:, cols].rearrange("p (c u e) -> p c u e", u=2, e=2),
+                op=ALU.add,
+            )
 
         def mix(b):
             g_codes, g_scales = g_of[b]
@@ -232,16 +240,16 @@ def tile_nonlocalblock_pa_t_kernel(
                 nc.vector.tensor_tensor(out=result[:, a, :], in0=bank[:], in1=x_of[b][:, a, :], op=ALU.add)
             nc.sync.dma_start(out=out[b].rearrange("(p a) h w -> p a (h w)", a=OUT_BLOCKS), in_=result[:])
 
-        def unload_g(banks):
-            g_raw = work.tile([P, CH * PACK], BF16)
-            for half in range(2):
-                unload_half(banks[half], g_raw, half)
-            return g_raw
+        def new_g():
+            g_bf = work.tile([P, CH * PACK], BF16, align_bytes=64)
+            return g_bf
 
         def live(b):
             return 0 <= b < MAPS
 
-        g_raw_of = {0: unload_g([flip_half(gproj_of[0], half) for half in range(2)])}
+        g_bf_of = {0: new_g()}
+        for half in range(2):
+            add_decoder(flip_half(gproj_of[0], half), g_bf_of[0], half)
         y_bf_of = {}
 
         for k in range(MAPS + 2):
@@ -249,27 +257,28 @@ def tile_nonlocalblock_pa_t_kernel(
                 load_map(k + 2)
             banks = []
             if live(k):
+                if live(k + 1):
+                    g_bf_of[k + 1] = new_g()
                 for t in range(PACK):
                     softmax_block(k, t)
                     if PACK * k + t + AHEAD < PACK * MAPS:
                         scores_block(PACK * k + t + AHEAD)
                     if t < 2 and live(k + 1):
                         banks.append(flip_half(gproj_of[k + 1], t))
+                    if t >= 2 and live(k + 1):
+                        add_decoder(banks[t - 2], g_bf_of[k + 1], t - 2)
                 invert_sums(k, 0)
             if live(k - 2):
                 y_of[k - 2] = quantise("y", y_bf_of[k - 2][:].rearrange("p i t -> p (i t)"))
             if live(k):
-                g_bf = add_decoder(g_raw_of[k])
                 invert_sums(k, 2)
                 attn_rows = scale_rows(k)
             if live(k - 2):
                 project(k - 2)
             if live(k):
-                g_of[k] = quantise("g", g_bf[:])
+                g_of[k] = quantise("g", g_bf_of[k][:])
             if live(k - 1):
                 y_bf_of[k - 1] = mix(k - 1)
-            if live(k + 1):
-                g_raw_of[k + 1] = unload_g(banks)
             if live(k):
                 attn_bf = regroup(attn_rows)
                 attn_of[k] = quantise("attn", attn_bf[:].rearrange("p i t -> p (i t)"))

@@ -21,7 +21,7 @@ PACK = 4
 CHUNKS = CH // P
 OUT_BLOCKS = OUT_CH // P
 POS_ON_TENSOR = 2
-AHEAD = 3
+AHEAD = 2
 
 FLOPS = 2 * MAPS * (2 * POS * POS * CH + OUT_CH * CH * POS)
 
@@ -34,7 +34,7 @@ def tile_nonlocalblock_pa_t_kernel(
         const = ctx.enter_context(tc.tile_pool(name="const", bufs=1))
         loads = ctx.enter_context(tc.tile_pool(name="loads", bufs=3))
         work = ctx.enter_context(tc.tile_pool(name="work", bufs=2))
-        psum_scores = ctx.enter_context(tc.psum_pool(name="psum_scores", bufs=AHEAD))
+        psum_scores = ctx.enter_context(tc.psum_pool(name="psum_scores", bufs=AHEAD + 1))
         psum_flip = ctx.enter_context(tc.psum_pool(name="psum_flip", bufs=2))
         psum_mx = ctx.enter_context(tc.psum_pool(name="psum_mx", bufs=3))
 
@@ -43,11 +43,15 @@ def tile_nonlocalblock_pa_t_kernel(
         ident_bf = const.tile([P, P], BF16)
         make_identity(nc, ident_bf[:])
 
+        ctx.enter_context(tc.manual_schedule())
+
         theta_of, phi_of, gproj_of, x_of = {}, {}, {}, {}
         scores_of = {}
+        soft_of, rows_of, attn_bf_of, g_bf_of, y_bf_of, result_of = {}, {}, {}, {}, {}, {}
         g_of, attn_of, y_of = {}, {}, {}
+        flip_of, bank_of = {}, {}
 
-        def load_map(b):
+        def load_scores_operands(b):
             phi_sb = loads.tile([P, CHUNKS, 2, P, 2], BF16)
             nc.sync.dma_start(
                 out=phi_sb[:].rearrange("p k u q e -> p (k u q e)"),
@@ -55,11 +59,17 @@ def tile_nonlocalblock_pa_t_kernel(
             )
             theta_sb = loads.tile([P, CHUNKS, POS], BF16)
             nc.sync.dma_start(out=theta_sb[:], in_=theta[b].rearrange("(p k) n -> p k n", k=CHUNKS))
+            phi_of[b], theta_of[b] = phi_sb, theta_sb
+
+        def load_g(b):
             gproj_sb = loads.tile([P, CHUNKS * POS], BF16)
             nc.sync.dma_start(out=gproj_sb[:], in_=g_proj[b].rearrange("(p k) n -> p (k n)", k=CHUNKS))
-            x_sb = loads.tile([P, OUT_BLOCKS, POS], BF16, bufs=5)
+            gproj_of[b] = gproj_sb
+
+        def load_x(b):
+            x_sb = loads.tile([P, OUT_BLOCKS, POS], BF16)
             nc.sync.dma_start(out=x_sb[:], in_=x[b].rearrange("(p a) h w -> p a (h w)", a=OUT_BLOCKS))
-            phi_of[b], theta_of[b], gproj_of[b], x_of[b] = phi_sb, theta_sb, gproj_sb, x_sb
+            x_of[b] = x_sb
 
         def flip_half(src, half):
             words = src[:].bitcast(F32)
@@ -79,14 +89,15 @@ def tile_nonlocalblock_pa_t_kernel(
 
         pos_sb = const.tile([P, PACK, POS], BF16)
         nc.sync.dma_start(out=pos_sb[:], in_=pos_embedding[0].rearrange("(a p) j -> p a j", p=P))
-        load_map(0)
+        load_scores_operands(0)
+        load_scores_operands(1)
         dec_sb = const.tile([P, CHUNKS * POS], BF16)
         nc.sync.dma_start(
             out=dec_sb[:], in_=pos_embedding_decoder[0].rearrange("(p k) h w -> p (k h w)", k=CHUNKS)
         )
+        load_g(0)
         w_sb = const.tile([P, OUT_BLOCKS * CH], BF16)
         nc.sync.dma_start(out=w_sb[:], in_=w_mask.rearrange("(p a) c -> p (a c)", a=OUT_BLOCKS))
-        load_map(1)
 
         pos_t = const.tile([P, PACK, POS], BF16)
         pos_words = pos_sb[:].rearrange("p a j -> p (a j)").bitcast(F32)
@@ -117,49 +128,58 @@ def tile_nonlocalblock_pa_t_kernel(
                 nc.tensor.matmul(out=acc[:], lhsT=ident_bf[:], rhs=pos_t[:, t, :], start=False, stop=True)
             scores_of[n] = acc
 
-        for n in range(AHEAD):
-            scores_block(n)
-
         dec_t = const.tile([P, CHUNKS * P * PACK], BF16)
-        for half in range(2):
-            unload_half(flip_half(dec_sb, half), dec_t, half)
 
         w_grouped = const.tile([P, OUT_CH * PACK], BF16, align_bytes=64)
         w_codes = const.tile([P, OUT_CH], U32, align_bytes=64)
         w_scales = const.tile([P, OUT_CH], U8, align_bytes=64)
-        w_words = w_sb[:].bitcast(F32)
-        bank = psum_flip.tile([P, OUT_BLOCKS, 2, P], F32, tag="flip")
-        for a in range(OUT_BLOCKS):
-            for u in range(2):
-                nc.tensor.transpose(
-                    bank[:, a, u, :], w_words[:, a * (CH // 2) + u : (a + 1) * (CH // 2) : 2], ident[:]
-                )
-        nc.scalar.copy(
-            out=w_grouped[:].bitcast(F32).rearrange("p (a r u) -> p a r u", a=OUT_BLOCKS, u=2),
-            in_=bank[:].rearrange("p a u r -> p a r u"),
-        )
-        nc.vector.quantize_mx(out=w_codes[:].bitcast(FP8X4), scales=w_scales[:], in_=w_grouped[:])
 
-        soft_of = {}
+        def prepare_w():
+            w_words = w_sb[:].bitcast(F32)
+            bank = psum_flip.tile([P, OUT_BLOCKS, 2, P], F32, tag="flip")
+            for a in range(OUT_BLOCKS):
+                for u in range(2):
+                    nc.tensor.transpose(
+                        bank[:, a, u, :], w_words[:, a * (CH // 2) + u : (a + 1) * (CH // 2) : 2], ident[:]
+                    )
+            nc.scalar.copy(
+                out=w_grouped[:].bitcast(F32).rearrange("p (a r u) -> p a r u", a=OUT_BLOCKS, u=2),
+                in_=bank[:].rearrange("p a u r -> p a r u"),
+            )
+            nc.vector.quantize_mx(out=w_codes[:].bitcast(FP8X4), scales=w_scales[:], in_=w_grouped[:])
 
-        def softmax_block(b, t):
-            if t == 0:
-                shifted = work.tile([P, PACK, POS], F32)
-                expd = work.tile([P, PACK, POS], F32)
-                neg_max = work.tile([P, PACK], F32)
-                row_sum = work.tile([P, PACK], F32)
-                inv_sum = work.tile([P, PACK], F32)
-                soft_of[b] = (shifted, expd, neg_max, row_sum, inv_sum)
-            shifted, expd, neg_max, row_sum = soft_of[b][:4]
+        def new_softmax(b):
+            shifted = work.tile([P, PACK, POS], F32)
+            expd = work.tile([P, PACK, POS], F32)
+            neg_max = work.tile([P, PACK], F32)
+            row_sum = work.tile([P, PACK], F32)
+            inv_sum = work.tile([P, PACK], F32)
+            soft_of[b] = (shifted, expd, neg_max, row_sum, inv_sum)
+            attn_rows = work.tile([P, PACK, POS], BF16)
+            rows_of[b] = attn_rows
+
+        def with_pos(b, t):
             if pos_on_tensor(t):
-                with_pos = scores_of[PACK * b + t][:]
-            else:
-                with_pos = shifted[:, t, :]
-                nc.vector.tensor_tensor(out=with_pos, in0=scores_of[PACK * b + t][:], in1=pos_t[:, t, :], op=ALU.add)
-            nc.vector.tensor_reduce(out=neg_max[:, t : t + 1], in_=with_pos, axis=AXIS.X, op=ALU.max, negate=True)
+                return scores_of[PACK * b + t][:]
+            return soft_of[b][0][:, t, :]
+
+        def add_pos(b, t):
+            if not pos_on_tensor(t):
+                nc.vector.tensor_tensor(
+                    out=with_pos(b, t), in0=scores_of[PACK * b + t][:], in1=pos_t[:, t, :], op=ALU.add
+                )
+
+        def row_max(b, t):
+            neg_max = soft_of[b][2]
+            nc.vector.tensor_reduce(
+                out=neg_max[:, t : t + 1], in_=with_pos(b, t), axis=AXIS.X, op=ALU.max, negate=True
+            )
+
+        def exponentials(b, t):
+            expd, neg_max, row_sum = soft_of[b][1:4]
             nc.scalar.activation(
                 out=expd[:, t, :],
-                in_=with_pos,
+                in_=with_pos(b, t),
                 func=ACT.Exp,
                 bias=neg_max[:, t : t + 1],
                 scale=1.0,
@@ -170,20 +190,31 @@ def tile_nonlocalblock_pa_t_kernel(
             row_sum, inv_sum = soft_of[b][3], soft_of[b][4]
             nc.vector.reciprocal(out=inv_sum[:, first : first + 2], in_=row_sum[:, first : first + 2])
 
-        def scale_rows(b):
+        def scale_rows(b, t):
             expd, inv_sum = soft_of[b][1], soft_of[b][4]
-            attn_rows = work.tile([P, PACK, POS], BF16)
-            for t in range(PACK):
-                nc.scalar.activation(out=attn_rows[:, t, :], in_=expd[:, t, :], func=ACT.Copy, scale=inv_sum[:, t : t + 1])
-            return attn_rows
-
-        def regroup(attn_rows):
-            attn_bf = work.tile([P, POS, PACK], BF16, align_bytes=64)
-            nc.vector.tensor_copy(
-                out=attn_bf[:].rearrange("p (c i) t -> p c t i", i=4),
-                in_=attn_rows[:].rearrange("p t (c i) -> p c t i", i=4),
+            nc.scalar.activation(
+                out=rows_of[b][:, t, :], in_=expd[:, t, :], func=ACT.Copy, scale=inv_sum[:, t : t + 1]
             )
-            return attn_bf
+
+        def regroup(b):
+            attn_bf = work.tile([P, POS, PACK], BF16, align_bytes=64)
+            attn_bf_of[b] = attn_bf
+            if b == MAPS - 1:
+                nc.vector.tensor_copy(
+                    out=attn_bf[:].rearrange("p (c i) t -> p c t i", i=4),
+                    in_=rows_of[b][:].rearrange("p t (c i) -> p c t i", i=4),
+                )
+                return
+            for r in range(POS // P):
+                cols = slice(r * P, (r + 1) * P)
+                nc.gpsimd.tensor_scalar(
+                    out=attn_bf[:, cols, :].rearrange("p (c i) t -> p c t i", i=4),
+                    in0=rows_of[b][:, :, cols].rearrange("p t (c i) -> p c t i", i=4),
+                    scalar1=1.0,
+                    scalar2=0.0,
+                    op0=ALU.mult,
+                    op1=ALU.add,
+                )
 
         def quantise(what, grouped):
             codes = work.tile([P, POS], U32, align_bytes=64, name=what + "_codes", tag=what + "_codes")
@@ -191,7 +222,11 @@ def tile_nonlocalblock_pa_t_kernel(
             nc.vector.quantize_mx(out=codes[:].bitcast(FP8X4), scales=scales[:], in_=grouped)
             return codes, scales
 
-        def add_decoder(bank, g_bf, half):
+        def add_decoder(b, half):
+            if half == 0:
+                g_bf = work.tile([P, CH * PACK], BF16, align_bytes=64)
+                g_bf_of[b] = g_bf
+            g_bf, bank = g_bf_of[b], flip_of[b, half]
             cols = slice(half * CH * PACK // 2, (half + 1) * CH * PACK // 2)
             pairs = bank[:].rearrange("p u h c -> p (u h c)").bitcast(BF16)
             nc.vector.tensor_tensor(
@@ -201,30 +236,33 @@ def tile_nonlocalblock_pa_t_kernel(
                 op=ALU.add,
             )
 
-        def mix(b):
+        def mix(b, r):
             g_codes, g_scales = g_of[b]
             a_codes, a_scales = attn_of[b]
-            y_bf = work.tile([P, POS, PACK], BF16, align_bytes=64)
-            for r in range(POS // P):
-                cols = slice(r * P, (r + 1) * P)
-                bank = psum_mx.tile([P, PACK, P], F32, tag="mx")
-                for t in range(PACK):
-                    group = slice(t * P, (t + 1) * P)
-                    nc.tensor.matmul_mx(
-                        out=bank[:, t, :],
-                        lhsT=g_codes[:, group].bitcast(FP8X4),
-                        lhsT_scale=g_scales[:, group],
-                        rhs=a_codes[:, cols].bitcast(FP8X4),
-                        rhs_scale=a_scales[:, cols],
-                        start=True,
-                        stop=True,
-                    )
-                nc.scalar.copy(out=y_bf[:, cols, :], in_=bank[:].rearrange("p t i -> p i t"))
-            return y_bf
+            cols = slice(r * P, (r + 1) * P)
+            bank = psum_mx.tile([P, PACK, P], F32, tag="mx")
+            for t in range(PACK):
+                group = slice(t * P, (t + 1) * P)
+                nc.tensor.matmul_mx(
+                    out=bank[:, t, :],
+                    lhsT=g_codes[:, group].bitcast(FP8X4),
+                    lhsT_scale=g_scales[:, group],
+                    rhs=a_codes[:, cols].bitcast(FP8X4),
+                    rhs_scale=a_scales[:, cols],
+                    start=True,
+                    stop=True,
+                )
+            bank_of["y", b, r] = bank
+
+        def unload_y(b, r):
+            if r == 0:
+                y_bf = work.tile([P, POS, PACK], BF16, align_bytes=64)
+                y_bf_of[b] = y_bf
+            cols = slice(r * P, (r + 1) * P)
+            nc.scalar.copy(out=y_bf_of[b][:, cols, :], in_=bank_of["y", b, r][:].rearrange("p t i -> p i t"))
 
         def project(b):
             y_codes, y_scales = y_of[b]
-            result = work.tile([P, OUT_BLOCKS, POS], F32)
             for a in range(OUT_BLOCKS):
                 rows = slice(a * P, (a + 1) * P)
                 bank = psum_mx.tile([P, POS], F32, tag="mx")
@@ -237,48 +275,98 @@ def tile_nonlocalblock_pa_t_kernel(
                     start=True,
                     stop=True,
                 )
-                nc.vector.tensor_tensor(out=result[:, a, :], in0=bank[:], in1=x_of[b][:, a, :], op=ALU.add)
-            nc.sync.dma_start(out=out[b].rearrange("(p a) h w -> p a (h w)", a=OUT_BLOCKS), in_=result[:])
+                bank_of["out", b, a] = bank
 
-        def new_g():
-            g_bf = work.tile([P, CH * PACK], BF16, align_bytes=64)
-            return g_bf
+        def add_x(b, a):
+            if a == 0:
+                result = work.tile([P, OUT_BLOCKS, POS], F32)
+                result_of[b] = result
+            result = result_of[b]
+            nc.vector.tensor_tensor(
+                out=result[:, a, :], in0=bank_of["out", b, a][:], in1=x_of[b][:, a, :], op=ALU.add
+            )
+            if a == OUT_BLOCKS - 1:
+                nc.sync.dma_start(out=out[b].rearrange("(p a) h w -> p a (h w)", a=OUT_BLOCKS), in_=result[:])
 
-        def live(b):
-            return 0 <= b < MAPS
+        def due(n, offset):
+            b, rest = divmod(n - offset, PACK)
+            return b if rest == 0 and 0 <= b < MAPS else -1
 
-        g_bf_of = {0: new_g()}
-        for half in range(2):
-            add_decoder(flip_half(gproj_of[0], half), g_bf_of[0], half)
-        y_bf_of = {}
+        for n in range(AHEAD):
+            scores_block(n)
 
-        for k in range(MAPS + 2):
-            if live(k + 2):
-                load_map(k + 2)
-            banks = []
-            if live(k):
-                if live(k + 1):
-                    g_bf_of[k + 1] = new_g()
-                for t in range(PACK):
-                    softmax_block(k, t)
-                    if PACK * k + t + AHEAD < PACK * MAPS:
-                        scores_block(PACK * k + t + AHEAD)
-                    if t < 2 and live(k + 1):
-                        banks.append(flip_half(gproj_of[k + 1], t))
-                    if t >= 2 and live(k + 1):
-                        add_decoder(banks[t - 2], g_bf_of[k + 1], t - 2)
-                invert_sums(k, 0)
-            if live(k - 2):
-                y_of[k - 2] = quantise("y", y_bf_of[k - 2][:].rearrange("p i t -> p (i t)"))
-            if live(k):
-                invert_sums(k, 2)
-                attn_rows = scale_rows(k)
-            if live(k - 2):
-                project(k - 2)
-            if live(k):
-                g_of[k] = quantise("g", g_bf_of[k][:])
-            if live(k - 1):
-                y_bf_of[k - 1] = mix(k - 1)
-            if live(k):
-                attn_bf = regroup(attn_rows)
-                attn_of[k] = quantise("attn", attn_bf[:].rearrange("p i t -> p (i t)"))
+        for n in range(PACK * MAPS + 17):
+            k, t = divmod(n, PACK)
+            busy = n < PACK * MAPS
+            if t == 0:
+                if k + 2 < MAPS:
+                    load_scores_operands(k + 2)
+                if k + 1 < MAPS:
+                    load_g(k + 1)
+                if 0 <= k - 2 < MAPS:
+                    load_x(k - 2)
+                if busy:
+                    new_softmax(k)
+            if t % 2 == 0:
+                b = due(n, 8)
+                if b >= 0:
+                    g_of[b] = quantise("g", g_bf_of[b][:])
+                if busy:
+                    add_pos(k, t)
+                for first, offset in ((0, 2), (2, 4)):
+                    b = due(n, offset)
+                    if b >= 0:
+                        invert_sums(b, first)
+                b = due(n, 16)
+                if b >= 0:
+                    add_x(b, 1)
+            for r in range(POS // P):
+                b = due(n, 10 + r)
+                if b >= 0:
+                    unload_y(b, r)
+            for block in range(PACK):
+                b = due(n, 2 + block)
+                if b >= 0:
+                    scale_rows(b, block)
+            b = due(n, 6)
+            if b >= 0:
+                regroup(b)
+            if t % 2 == 0:
+                b = due(n, 14)
+                if b >= 0:
+                    y_of[b] = quantise("y", y_bf_of[b][:].rearrange("p i t -> p (i t)"))
+                if busy:
+                    row_max(k, t)
+            else:
+                if busy:
+                    row_max(k, t)
+                b = due(n, 9)
+                if b >= 0:
+                    attn_of[b] = quantise("attn", attn_bf_of[b][:].rearrange("p i t -> p (i t)"))
+                b = due(n, 15)
+                if b >= 0:
+                    add_x(b, 0)
+                for half, offset in ((0, 5), (1, 7)):
+                    b = due(n, offset)
+                    if b >= 0:
+                        add_decoder(b, half)
+            if busy:
+                exponentials(k, t)
+            if n + AHEAD < PACK * MAPS:
+                scores_block(n + AHEAD)
+            if n == 2:
+                for half in range(2):
+                    unload_half(flip_half(dec_sb, half), dec_t, half)
+            if n == 8:
+                prepare_w()
+            for half, offset in ((0, 4), (1, 6)):
+                b = due(n, offset)
+                if b >= 0:
+                    flip_of[b, half] = flip_half(gproj_of[b], half)
+            for r in range(POS // P):
+                b = due(n, 9 + r)
+                if b >= 0:
+                    mix(b, r)
+            b = due(n, 14)
+            if b >= 0:
+                project(b)

@@ -295,7 +295,7 @@ def tile_nonlocalblock_pa_t_kernel(
         for n in range(AHEAD):
             scores_block(n)
 
-        for n in range(PACK * MAPS + 17):
+        for n in range(PACK * MAPS + 20):
             k, t = divmod(n, PACK)
             busy = n < PACK * MAPS
             if t == 0:
@@ -303,70 +303,64 @@ def tile_nonlocalblock_pa_t_kernel(
                     load_scores_operands(k + 2)
                 if k + 1 < MAPS:
                     load_g(k + 1)
-                if 0 <= k - 2 < MAPS:
-                    load_x(k - 2)
+                if 0 <= k - 3 < MAPS:
+                    load_x(k - 3)
                 if busy:
                     new_softmax(k)
-            if t % 2 == 0:
-                b = due(n, 8)
-                if b >= 0:
-                    g_of[b] = quantise("g", g_bf_of[b][:])
-                if busy:
-                    add_pos(k, t)
-                for first, offset in ((0, 2), (2, 4)):
-                    b = due(n, offset)
-                    if b >= 0:
-                        invert_sums(b, first)
-                b = due(n, 16)
-                if b >= 0:
-                    add_x(b, 1)
+            if 0 < n <= PACK * MAPS:
+                exponentials(*divmod(n - 1, PACK))
             for r in range(POS // P):
-                b = due(n, 10 + r)
+                b = due(n, 12 + r)
                 if b >= 0:
                     unload_y(b, r)
-            for block in range(PACK):
-                b = due(n, 2 + block)
+            for block, offset in enumerate((3, 4, 5, 5)):
+                b = due(n, offset)
                 if b >= 0:
                     scale_rows(b, block)
-            b = due(n, 6)
-            if b >= 0:
-                regroup(b)
-            if t % 2 == 0:
-                b = due(n, 14)
-                if b >= 0:
-                    y_of[b] = quantise("y", y_bf_of[b][:].rearrange("p i t -> p (i t)"))
-                if busy:
-                    row_max(k, t)
-            else:
-                if busy:
-                    row_max(k, t)
-                b = due(n, 9)
-                if b >= 0:
-                    attn_of[b] = quantise("attn", attn_bf_of[b][:].rearrange("p i t -> p (i t)"))
-                b = due(n, 15)
-                if b >= 0:
-                    add_x(b, 0)
-                for half, offset in ((0, 5), (1, 7)):
-                    b = due(n, offset)
-                    if b >= 0:
-                        add_decoder(b, half)
+                    if block == PACK - 1:
+                        regroup(b)
             if busy:
-                exponentials(k, t)
-            if n + AHEAD < PACK * MAPS:
+                add_pos(k, t)
+            b = due(n, 11)
+            if b >= 0:
+                attn_of[b] = quantise("attn", attn_bf_of[b][:].rearrange("p i t -> p (i t)"))
+            b = due(n, 10)
+            if b >= 0:
+                g_of[b] = quantise("g", g_bf_of[b][:])
+            b = due(n, 16)
+            if b >= 0:
+                y_of[b] = quantise("y", y_bf_of[b][:].rearrange("p i t -> p (i t)"))
+            for a, offset in ((0, 17), (1, 19)):
+                b = due(n, offset)
+                if b >= 0:
+                    add_x(b, a)
+            for half, offset in ((0, 7), (1, 9)):
+                b = due(n, offset)
+                if b >= 0:
+                    add_decoder(b, half)
+            if busy:
+                row_max(k, t)
+            for first, offset in ((0, 2), (2, 4)):
+                b = due(n, offset)
+                if b >= 0:
+                    invert_sums(b, first)
+            if t % 2 == 1 and n + AHEAD < PACK * MAPS:
                 scores_block(n + AHEAD)
             if n == 2:
                 for half in range(2):
                     unload_half(flip_half(dec_sb, half), dec_t, half)
             if n == 8:
                 prepare_w()
-            for half, offset in ((0, 4), (1, 6)):
-                b = due(n, offset)
-                if b >= 0:
+            b = due(n, 6)
+            if b >= 0:
+                for half in range(2):
                     flip_of[b, half] = flip_half(gproj_of[b], half)
             for r in range(POS // P):
-                b = due(n, 9 + r)
+                b = due(n, 11 + r)
                 if b >= 0:
                     mix(b, r)
-            b = due(n, 14)
+            if t % 2 == 0 and n + AHEAD < PACK * MAPS:
+                scores_block(n + AHEAD)
+            b = due(n, 16)
             if b >= 0:
                 project(b)

@@ -208,8 +208,8 @@ def tile_nonlocalblock_pa_t_kernel(
             for r in range(POS // P):
                 cols = slice(r * P, (r + 1) * P)
                 nc.gpsimd.tensor_scalar(
-                    out=attn_bf[:, cols, :].rearrange("p (c i) t -> p c t i", i=4),
-                    in0=rows_of[b][:, :, cols].rearrange("p t (c i) -> p c t i", i=4),
+                    out=attn_bf[:, cols, :],
+                    in0=rows_of[b][:, :, cols].rearrange("p t i -> p i t"),
                     scalar1=1.0,
                     scalar2=0.0,
                     op0=ALU.mult,

@@ -20,7 +20,7 @@ P = 128
 PACK = 4
 CHUNKS = CH // P
 OUT_BLOCKS = OUT_CH // P
-POS_ON_TENSOR = 2
+POS_ALL_ON_TENSOR = 3
 AHEAD = 2
 
 FLOPS = 2 * MAPS * (2 * POS * POS * CH + OUT_CH * CH * POS)
@@ -67,7 +67,7 @@ def tile_nonlocalblock_pa_t_kernel(
             gproj_of[b] = gproj_sb
 
         def load_x(b):
-            x_sb = loads.tile([P, OUT_BLOCKS, POS], BF16)
+            x_sb = loads.tile([P, OUT_BLOCKS, POS], BF16, bufs=5)
             nc.sync.dma_start(out=x_sb[:], in_=x[b].rearrange("(p a) h w -> p a (h w)", a=OUT_BLOCKS))
             x_of[b] = x_sb
 
@@ -109,8 +109,8 @@ def tile_nonlocalblock_pa_t_kernel(
             pairs = bank[:].rearrange("p a i -> p (a i)").bitcast(BF16)
             nc.vector.tensor_copy(out=pos_t[:, 2 * u : 2 * u + 2, :], in_=pairs.rearrange("p (i e) -> p e i", e=2))
 
-        def pos_on_tensor(t):
-            return t % 2 == 1 and t // 2 < POS_ON_TENSOR
+        def pos_on_tensor(b, t):
+            return t % 2 == 1 or b >= MAPS - POS_ALL_ON_TENSOR
 
         def scores_block(n):
             b, t = divmod(n, PACK)
@@ -122,9 +122,9 @@ def tile_nonlocalblock_pa_t_kernel(
                     lhsT=phi_of[b][:, k, u, :, e],
                     rhs=theta_of[b][:, k, :],
                     start=(k == 0),
-                    stop=(k == CHUNKS - 1 and not pos_on_tensor(t)),
+                    stop=(k == CHUNKS - 1 and not pos_on_tensor(b, t)),
                 )
-            if pos_on_tensor(t):
+            if pos_on_tensor(b, t):
                 nc.tensor.matmul(out=acc[:], lhsT=ident_bf[:], rhs=pos_t[:, t, :], start=False, stop=True)
             scores_of[n] = acc
 
@@ -159,12 +159,12 @@ def tile_nonlocalblock_pa_t_kernel(
             rows_of[b] = attn_rows
 
         def with_pos(b, t):
-            if pos_on_tensor(t):
+            if pos_on_tensor(b, t):
                 return scores_of[PACK * b + t][:]
             return soft_of[b][0][:, t, :]
 
         def add_pos(b, t):
-            if not pos_on_tensor(t):
+            if not pos_on_tensor(b, t):
                 nc.vector.tensor_tensor(
                     out=with_pos(b, t), in0=scores_of[PACK * b + t][:], in1=pos_t[:, t, :], op=ALU.add
                 )
@@ -196,10 +196,10 @@ def tile_nonlocalblock_pa_t_kernel(
                 out=rows_of[b][:, t, :], in_=expd[:, t, :], func=ACT.Copy, scale=inv_sum[:, t : t + 1]
             )
 
-        def regroup(b):
+        def regroup(b, engine):
             attn_bf = work.tile([P, POS, PACK], BF16, align_bytes=64)
             attn_bf_of[b] = attn_bf
-            if b == MAPS - 1:
+            if engine is nc.vector:
                 nc.vector.tensor_copy(
                     out=attn_bf[:].rearrange("p (c i) t -> p c t i", i=4),
                     in_=rows_of[b][:].rearrange("p t (c i) -> p c t i", i=4),
@@ -236,11 +236,11 @@ def tile_nonlocalblock_pa_t_kernel(
                 op=ALU.add,
             )
 
-        def mix(b, r):
+        def mix(b, r, pool=psum_mx, tag="mx"):
             g_codes, g_scales = g_of[b]
             a_codes, a_scales = attn_of[b]
             cols = slice(r * P, (r + 1) * P)
-            bank = psum_mx.tile([P, PACK, P], F32, tag="mx")
+            bank = pool.tile([P, PACK, P], F32, tag=tag)
             for t in range(PACK):
                 group = slice(t * P, (t + 1) * P)
                 nc.tensor.matmul_mx(
@@ -254,18 +254,18 @@ def tile_nonlocalblock_pa_t_kernel(
                 )
             bank_of["y", b, r] = bank
 
-        def unload_y(b, r):
+        def unload_y(b, r, copy=nc.scalar.copy):
             if r == 0:
                 y_bf = work.tile([P, POS, PACK], BF16, align_bytes=64)
                 y_bf_of[b] = y_bf
             cols = slice(r * P, (r + 1) * P)
-            nc.scalar.copy(out=y_bf_of[b][:, cols, :], in_=bank_of["y", b, r][:].rearrange("p t i -> p i t"))
+            copy(out=y_bf_of[b][:, cols, :], in_=bank_of["y", b, r][:].rearrange("p t i -> p i t"))
 
-        def project(b):
+        def project(b, pool=psum_mx, tag="mx"):
             y_codes, y_scales = y_of[b]
             for a in range(OUT_BLOCKS):
                 rows = slice(a * P, (a + 1) * P)
-                bank = psum_mx.tile([P, POS], F32, tag="mx")
+                bank = pool.tile([P, POS], F32, tag=tag)
                 nc.tensor.matmul_mx(
                     out=bank[:],
                     lhsT=w_codes[:, rows].bitcast(FP8X4),
@@ -279,38 +279,50 @@ def tile_nonlocalblock_pa_t_kernel(
 
         def add_x(b, a):
             if a == 0:
-                result = work.tile([P, OUT_BLOCKS, POS], F32)
+                result = work.tile([P, OUT_BLOCKS, POS], F32, bufs=3)
                 result_of[b] = result
             result = result_of[b]
             nc.vector.tensor_tensor(
                 out=result[:, a, :], in0=bank_of["out", b, a][:], in1=x_of[b][:, a, :], op=ALU.add
             )
-            if a == OUT_BLOCKS - 1:
-                nc.sync.dma_start(out=out[b].rearrange("(p a) h w -> p a (h w)", a=OUT_BLOCKS), in_=result[:])
+            rows = out[b].rearrange("(p a) h w -> p a (h w)", a=OUT_BLOCKS)
+            if b == MAPS - 1:
+                nc.sync.dma_start(out=rows[:, a, :], in_=result[:, a, :])
+            elif a == OUT_BLOCKS - 1:
+                nc.sync.dma_start(out=rows, in_=result[:])
 
         def due(n, offset):
             b, rest = divmod(n - offset, PACK)
             return b if rest == 0 and 0 <= b < MAPS else -1
 
+        def quantise_attn(b):
+            attn_of[b] = quantise("attn", attn_bf_of[b][:].rearrange("p i t -> p (i t)"))
+
+        def quantise_g(b):
+            g_of[b] = quantise("g", g_bf_of[b][:])
+
+        def quantise_y(b):
+            y_of[b] = quantise("y", y_bf_of[b][:].rearrange("p i t -> p (i t)"))
+
         for n in range(AHEAD):
             scores_block(n)
 
-        for n in range(PACK * MAPS + 20):
+        for n in range(PACK * MAPS):
             k, t = divmod(n, PACK)
-            busy = n < PACK * MAPS
             if t == 0:
                 if k + 2 < MAPS:
                     load_scores_operands(k + 2)
                 if k + 1 < MAPS:
                     load_g(k + 1)
-                if 0 <= k - 3 < MAPS:
-                    load_x(k - 3)
-                if busy:
-                    new_softmax(k)
-            if 0 < n <= PACK * MAPS:
+                if k >= 1:
+                    load_x(k - 1)
+                if k == MAPS - 1:
+                    load_x(k)
+                new_softmax(k)
+            if n > 0:
                 exponentials(*divmod(n - 1, PACK))
             for r in range(POS // P):
-                b = due(n, 12 + r)
+                b = due(n, 10 + r)
                 if b >= 0:
                     unload_y(b, r)
             for block, offset in enumerate((3, 4, 5, 5)):
@@ -318,28 +330,28 @@ def tile_nonlocalblock_pa_t_kernel(
                 if b >= 0:
                     scale_rows(b, block)
                     if block == PACK - 1:
-                        regroup(b)
-            if busy:
-                add_pos(k, t)
-            b = due(n, 11)
+                        regroup(b, nc.gpsimd)
+            add_pos(k, t)
+            b = due(n, 9)
             if b >= 0:
-                attn_of[b] = quantise("attn", attn_bf_of[b][:].rearrange("p i t -> p (i t)"))
-            b = due(n, 10)
+                quantise_attn(b)
+            b = due(n, 8)
             if b >= 0:
-                g_of[b] = quantise("g", g_bf_of[b][:])
-            b = due(n, 16)
+                quantise_g(b)
+            b = due(n, 14)
             if b >= 0:
-                y_of[b] = quantise("y", y_bf_of[b][:].rearrange("p i t -> p (i t)"))
-            for a, offset in ((0, 17), (1, 19)):
-                b = due(n, offset)
-                if b >= 0:
-                    add_x(b, a)
-            for half, offset in ((0, 7), (1, 9)):
+                quantise_y(b)
+            b = due(n, 17)
+            if b >= 0:
+                add_x(b, 1)
+            for half, offset in ((0, 5), (1, 7)):
                 b = due(n, offset)
                 if b >= 0:
                     add_decoder(b, half)
-            if busy:
-                row_max(k, t)
+            b = due(n, 15)
+            if b >= 0:
+                add_x(b, 0)
+            row_max(k, t)
             for first, offset in ((0, 2), (2, 4)):
                 b = due(n, offset)
                 if b >= 0:
@@ -351,16 +363,58 @@ def tile_nonlocalblock_pa_t_kernel(
                     unload_half(flip_half(dec_sb, half), dec_t, half)
             if n == 8:
                 prepare_w()
-            b = due(n, 6)
+            b = due(n, 4)
             if b >= 0:
                 for half in range(2):
                     flip_of[b, half] = flip_half(gproj_of[b], half)
             for r in range(POS // P):
-                b = due(n, 11 + r)
+                b = due(n, 9 + r)
                 if b >= 0:
                     mix(b, r)
             if t % 2 == 0 and n + AHEAD < PACK * MAPS:
                 scores_block(n + AHEAD)
-            b = due(n, 16)
+            b = due(n, 14)
             if b >= 0:
                 project(b)
+
+        z = MAPS - 1
+        exponentials(z, 3)
+        mix(z - 2, 3)
+        for half in range(2):
+            flip_of[z, half] = flip_half(gproj_of[z], half)
+        quantise_g(z - 1)
+        quantise_attn(z - 1)
+        invert_sums(z, 2)
+        for block in range(1, PACK):
+            scale_rows(z, block)
+        add_decoder(z, 0)
+        add_x(z - 3, 1)
+        mix(z - 1, 0)
+        unload_y(z - 2, 2)
+        mix(z - 1, 1)
+        unload_y(z - 2, 3)
+        regroup(z, nc.vector)
+        add_decoder(z, 1)
+        quantise_attn(z)
+        quantise_g(z)
+        for r in range(POS // P):
+            if r >= 2:
+                mix(z - 1, r)
+            unload_y(z - 1, r)
+        for r in range(3):
+            mix(z, r, psum_scores, "scores")
+        quantise_y(z - 2)
+        mix(z, 3)
+        for r in range(3):
+            unload_y(z, r)
+        project(z - 2)
+        quantise_y(z - 1)
+        unload_y(z, 3, nc.vector.tensor_copy)
+        add_x(z - 2, 0)
+        quantise_y(z)
+        add_x(z - 2, 1)
+        project(z - 1, psum_scores, "scores")
+        project(z)
+        for b in (z - 1, z):
+            for a in range(OUT_BLOCKS):
+                add_x(b, a)

@@ -20,7 +20,7 @@ P = 128
 PACK = 4
 CHUNKS = CH // P
 OUT_BLOCKS = OUT_CH // P
-POS_ALL_ON_TENSOR = 3
+POS_ALL_ON_TENSOR = 1
 AHEAD = 2
 
 FLOPS = 2 * MAPS * (2 * POS * POS * CH + OUT_CH * CH * POS)
@@ -34,9 +34,8 @@ def tile_nonlocalblock_pa_t_kernel(
         const = ctx.enter_context(tc.tile_pool(name="const", bufs=1))
         loads = ctx.enter_context(tc.tile_pool(name="loads", bufs=3))
         work = ctx.enter_context(tc.tile_pool(name="work", bufs=2))
-        psum_scores = ctx.enter_context(tc.psum_pool(name="psum_scores", bufs=AHEAD + 1))
-        psum_flip = ctx.enter_context(tc.psum_pool(name="psum_flip", bufs=2))
-        psum_mx = ctx.enter_context(tc.psum_pool(name="psum_mx", bufs=3))
+        psum_scores = ctx.enter_context(tc.psum_pool(name="psum_scores", bufs=4))
+        psum_rest = ctx.enter_context(tc.psum_pool(name="psum_rest", bufs=4))
 
         ident = const.tile([P, P], F32)
         make_identity(nc, ident[:])
@@ -73,7 +72,7 @@ def tile_nonlocalblock_pa_t_kernel(
 
         def flip_half(src, half):
             words = src[:].bitcast(F32)
-            bank = psum_flip.tile([P, 2, 2, P], F32, tag="flip")
+            bank = psum_rest.tile([P, 2, 2, P], F32, tag="rest")
             for h in range(2):
                 for u in range(2):
                     first = (2 * half + h) * (POS // 2) + u * P
@@ -110,7 +109,7 @@ def tile_nonlocalblock_pa_t_kernel(
             nc.vector.tensor_copy(out=pos_t[:, 2 * u : 2 * u + 2, :], in_=pairs.rearrange("p (i e) -> p e i", e=2))
 
         def pos_on_tensor(b, t):
-            return t % 2 == 1 or b >= MAPS - POS_ALL_ON_TENSOR
+            return b > 0 and t % 2 == 1 or b >= MAPS - POS_ALL_ON_TENSOR
 
         def scores_block(n):
             b, t = divmod(n, PACK)
@@ -136,7 +135,7 @@ def tile_nonlocalblock_pa_t_kernel(
 
         def prepare_w():
             w_words = w_sb[:].bitcast(F32)
-            bank = psum_flip.tile([P, OUT_BLOCKS, 2, P], F32, tag="flip")
+            bank = psum_rest.tile([P, OUT_BLOCKS, 2, P], F32, tag="rest")
             for a in range(OUT_BLOCKS):
                 for u in range(2):
                     nc.tensor.transpose(
@@ -236,7 +235,7 @@ def tile_nonlocalblock_pa_t_kernel(
                 op=ALU.add,
             )
 
-        def mix(b, r, pool=psum_mx, tag="mx"):
+        def mix(b, r, pool=psum_rest, tag="rest"):
             g_codes, g_scales = g_of[b]
             a_codes, a_scales = attn_of[b]
             cols = slice(r * P, (r + 1) * P)
@@ -261,7 +260,7 @@ def tile_nonlocalblock_pa_t_kernel(
             cols = slice(r * P, (r + 1) * P)
             copy(out=y_bf_of[b][:, cols, :], in_=bank_of["y", b, r][:].rearrange("p t i -> p i t"))
 
-        def project(b, pool=psum_mx, tag="mx"):
+        def project(b, pool=psum_rest, tag="rest"):
             y_codes, y_scales = y_of[b]
             for a in range(OUT_BLOCKS):
                 rows = slice(a * P, (a + 1) * P)
@@ -277,19 +276,27 @@ def tile_nonlocalblock_pa_t_kernel(
                 )
                 bank_of["out", b, a] = bank
 
+        def new_result(b):
+            result = work.tile([P, OUT_BLOCKS, POS], F32, bufs=3)
+            result_of[b] = result
+
         def add_x(b, a):
-            if a == 0:
-                result = work.tile([P, OUT_BLOCKS, POS], F32, bufs=3)
-                result_of[b] = result
-            result = result_of[b]
             nc.vector.tensor_tensor(
-                out=result[:, a, :], in0=bank_of["out", b, a][:], in1=x_of[b][:, a, :], op=ALU.add
+                out=result_of[b][:, a, :], in0=bank_of["out", b, a][:], in1=x_of[b][:, a, :], op=ALU.add
             )
+
+        def unload_product(b, a):
+            nc.scalar.copy(out=result_of[b][:, a, :], in_=bank_of["out", b, a][:])
+
+        def add_x_later(b, a):
+            for half in range(2):
+                cols = slice(half * POS // 2, (half + 1) * POS // 2)
+                product = result_of[b][:, a, cols]
+                nc.gpsimd.tensor_tensor(out=product, in0=product, in1=x_of[b][:, a, cols], op=ALU.add)
+
+        def store(b, a=slice(0, OUT_BLOCKS)):
             rows = out[b].rearrange("(p a) h w -> p a (h w)", a=OUT_BLOCKS)
-            if b == MAPS - 1:
-                nc.sync.dma_start(out=rows[:, a, :], in_=result[:, a, :])
-            elif a == OUT_BLOCKS - 1:
-                nc.sync.dma_start(out=rows, in_=result[:])
+            nc.sync.dma_start(out=rows[:, a, :], in_=result_of[b][:, a, :])
 
         def due(n, offset):
             b, rest = divmod(n - offset, PACK)
@@ -325,6 +332,10 @@ def tile_nonlocalblock_pa_t_kernel(
                 b = due(n, 10 + r)
                 if b >= 0:
                     unload_y(b, r)
+            b = due(n, 15)
+            if b >= 0:
+                new_result(b)
+                unload_product(b, 1)
             for block, offset in enumerate((3, 4, 5, 5)):
                 b = due(n, offset)
                 if b >= 0:
@@ -338,20 +349,19 @@ def tile_nonlocalblock_pa_t_kernel(
             b = due(n, 8)
             if b >= 0:
                 quantise_g(b)
+            for half in range(2):
+                b = due(n, 5 + half)
+                if b >= 0:
+                    add_decoder(b, half)
             b = due(n, 14)
             if b >= 0:
                 quantise_y(b)
-            b = due(n, 17)
-            if b >= 0:
-                add_x(b, 1)
-            for half, offset in ((0, 5), (1, 7)):
-                b = due(n, offset)
-                if b >= 0:
-                    add_decoder(b, half)
+            row_max(k, t)
             b = due(n, 15)
             if b >= 0:
                 add_x(b, 0)
-            row_max(k, t)
+                add_x_later(b, 1)
+                store(b)
             for first, offset in ((0, 2), (2, 4)):
                 b = due(n, offset)
                 if b >= 0:
@@ -388,33 +398,35 @@ def tile_nonlocalblock_pa_t_kernel(
         for block in range(1, PACK):
             scale_rows(z, block)
         add_decoder(z, 0)
-        add_x(z - 3, 1)
-        mix(z - 1, 0)
         unload_y(z - 2, 2)
-        mix(z - 1, 1)
+        mix(z - 1, 0)
         unload_y(z - 2, 3)
-        regroup(z, nc.vector)
+        mix(z - 1, 1)
         add_decoder(z, 1)
-        quantise_attn(z)
+        regroup(z, nc.vector)
         quantise_g(z)
+        quantise_attn(z)
         for r in range(POS // P):
             if r >= 2:
                 mix(z - 1, r)
             unload_y(z - 1, r)
-        for r in range(3):
+        for r in range(POS // P):
             mix(z, r, psum_scores, "scores")
         quantise_y(z - 2)
-        mix(z, 3)
         for r in range(3):
             unload_y(z, r)
         project(z - 2)
         quantise_y(z - 1)
         unload_y(z, 3, nc.vector.tensor_copy)
+        new_result(z - 2)
         add_x(z - 2, 0)
         quantise_y(z)
         add_x(z - 2, 1)
-        project(z - 1, psum_scores, "scores")
-        project(z)
+        store(z - 2)
+        project(z - 1)
+        project(z, psum_scores, "scores")
         for b in (z - 1, z):
+            new_result(b)
             for a in range(OUT_BLOCKS):
                 add_x(b, a)
+                store(b, a)

@@ -20,7 +20,6 @@ P = 128
 PACK = 4
 CHUNKS = CH // P
 OUT_BLOCKS = OUT_CH // P
-POS_ALL_ON_TENSOR = 1
 AHEAD = 2
 
 FLOPS = 2 * MAPS * (2 * POS * POS * CH + OUT_CH * CH * POS)
@@ -50,14 +49,19 @@ def tile_nonlocalblock_pa_t_kernel(
         g_of, attn_of, y_of = {}, {}, {}
         flip_of, bank_of = {}, {}
 
-        def load_scores_operands(b):
+        def load_scores_operands(b, parts=1):
             phi_sb = loads.tile([P, CHUNKS, 2, P, 2], BF16)
-            nc.sync.dma_start(
-                out=phi_sb[:].rearrange("p k u q e -> p (k u q e)"),
-                in_=phi[b].rearrange("(p k) n -> p (k n)", k=CHUNKS),
-            )
             theta_sb = loads.tile([P, CHUNKS, POS], BF16)
-            nc.sync.dma_start(out=theta_sb[:], in_=theta[b].rearrange("(p k) n -> p k n", k=CHUNKS))
+            step = CHUNKS // parts
+            for first in range(0, CHUNKS, step):
+                chunks = slice(first, first + step)
+                nc.sync.dma_start(
+                    out=phi_sb[:, chunks].rearrange("p k u q e -> p k (u q e)"),
+                    in_=phi[b].rearrange("(p k) n -> p k n", k=CHUNKS)[:, chunks, :],
+                )
+                nc.sync.dma_start(
+                    out=theta_sb[:, chunks, :], in_=theta[b].rearrange("(p k) n -> p k n", k=CHUNKS)[:, chunks, :]
+                )
             phi_of[b], theta_of[b] = phi_sb, theta_sb
 
         def load_g(b):
@@ -86,9 +90,12 @@ def tile_nonlocalblock_pa_t_kernel(
                 out=dst_words.rearrange("p (c u) -> p c u", u=2), in_=bank[:].rearrange("p u h c -> p (h c) u")
             )
 
-        pos_sb = const.tile([P, PACK, POS], BF16)
-        nc.sync.dma_start(out=pos_sb[:], in_=pos_embedding[0].rearrange("(a p) j -> p a j", p=P))
-        load_scores_operands(0)
+        pos_rows = pos_embedding[0].rearrange("(a p) j -> p a j", p=P)
+        pos_low = const.tile([P, PACK, POS // 2], BF16)
+        pos_high = const.tile([P, PACK, POS // 2], BF16)
+        nc.sync.dma_start(out=pos_low[:], in_=pos_rows[:, :, : POS // 2])
+        load_scores_operands(0, parts=2)
+        nc.sync.dma_start(out=pos_high[:], in_=pos_rows[:, :, POS // 2 :])
         load_scores_operands(1)
         dec_sb = const.tile([P, CHUNKS * POS], BF16)
         nc.sync.dma_start(
@@ -99,23 +106,31 @@ def tile_nonlocalblock_pa_t_kernel(
         nc.sync.dma_start(out=w_sb[:], in_=w_mask.rearrange("(p a) c -> p (a c)", a=OUT_BLOCKS))
 
         pos_t = const.tile([P, PACK, POS], BF16)
-        pos_words = pos_sb[:].rearrange("p a j -> p (a j)").bitcast(F32)
-        for u in range(2):
-            bank = psum_scores.tile([P, PACK, P], F32, tag="scores")
+
+        def turn_pos(u, half, copy):
+            pos_words = half[:].rearrange("p a j -> p (a j)").bitcast(F32)
+            bank = psum_rest.tile([P, PACK, P], F32, tag="rest")
             for a in range(PACK):
-                first = a * (POS // 2) + u * P
-                nc.tensor.transpose(bank[:, a, :], pos_words[:, first : first + P], ident[:])
+                nc.tensor.transpose(bank[:, a, :], pos_words[:, a * P : (a + 1) * P], ident[:])
             pairs = bank[:].rearrange("p a i -> p (a i)").bitcast(BF16)
-            nc.vector.tensor_copy(out=pos_t[:, 2 * u : 2 * u + 2, :], in_=pairs.rearrange("p (i e) -> p e i", e=2))
+            copy(out=pos_t[:, 2 * u : 2 * u + 2, :], in_=pairs.rearrange("p (i e) -> p e i", e=2))
+
+        turn_pos(0, pos_low, nc.vector.tensor_copy)
 
         def pos_on_tensor(b, t):
-            return b > 0 and t % 2 == 1 or b >= MAPS - POS_ALL_ON_TENSOR
+            if b == 0:
+                return False
+            return b == MAPS - 1 or t % 2 == 1
 
-        def scores_block(n):
+        def scores_passes(n, chunks):
             b, t = divmod(n, PACK)
             u, e = divmod(t, 2)
-            acc = psum_scores.tile([P, POS], F32, tag="scores")
-            for k in range(CHUNKS):
+            if chunks[0] == 0:
+                acc = psum_scores.tile([P, POS], F32, tag="scores")
+                scores_of[n] = acc
+            acc = scores_of[n]
+            closed = chunks[-1] == CHUNKS - 1
+            for k in chunks:
                 nc.tensor.matmul(
                     out=acc[:],
                     lhsT=phi_of[b][:, k, u, :, e],
@@ -123,9 +138,11 @@ def tile_nonlocalblock_pa_t_kernel(
                     start=(k == 0),
                     stop=(k == CHUNKS - 1 and not pos_on_tensor(b, t)),
                 )
-            if pos_on_tensor(b, t):
+            if closed and pos_on_tensor(b, t):
                 nc.tensor.matmul(out=acc[:], lhsT=ident_bf[:], rhs=pos_t[:, t, :], start=False, stop=True)
-            scores_of[n] = acc
+
+        def scores_block(n):
+            scores_passes(n, range(CHUNKS))
 
         dec_t = const.tile([P, CHUNKS * P * PACK], BF16)
 
@@ -195,15 +212,20 @@ def tile_nonlocalblock_pa_t_kernel(
                 out=rows_of[b][:, t, :], in_=expd[:, t, :], func=ACT.Copy, scale=inv_sum[:, t : t + 1]
             )
 
-        def regroup(b, engine):
+        def scale_rows_on_gpsimd(b, t):
+            expd, inv_sum = soft_of[b][1], soft_of[b][4]
+            nc.gpsimd.tensor_scalar(
+                out=rows_of[b][:, t, :],
+                in0=expd[:, t, :],
+                scalar1=inv_sum[:, t : t + 1],
+                scalar2=0.0,
+                op0=ALU.mult,
+                op1=ALU.add,
+            )
+
+        def regroup(b):
             attn_bf = work.tile([P, POS, PACK], BF16, align_bytes=64)
             attn_bf_of[b] = attn_bf
-            if engine is nc.vector:
-                nc.vector.tensor_copy(
-                    out=attn_bf[:].rearrange("p (c i) t -> p c t i", i=4),
-                    in_=rows_of[b][:].rearrange("p t (c i) -> p c t i", i=4),
-                )
-                return
             for r in range(POS // P):
                 cols = slice(r * P, (r + 1) * P)
                 nc.gpsimd.tensor_scalar(
@@ -214,6 +236,14 @@ def tile_nonlocalblock_pa_t_kernel(
                     op0=ALU.mult,
                     op1=ALU.add,
                 )
+
+        def regroup_on_vector(b):
+            attn_bf = work.tile([P, POS, PACK], BF16, align_bytes=64)
+            attn_bf_of[b] = attn_bf
+            nc.vector.tensor_copy(
+                out=attn_bf[:].rearrange("p (c i) t -> p c t i", i=4),
+                in_=rows_of[b][:].rearrange("p t (c i) -> p c t i", i=4),
+            )
 
         def quantise(what, grouped):
             codes = work.tile([P, POS], U32, align_bytes=64, name=what + "_codes", tag=what + "_codes")
@@ -277,7 +307,7 @@ def tile_nonlocalblock_pa_t_kernel(
                 bank_of["out", b, a] = bank
 
         def new_result(b):
-            result = work.tile([P, OUT_BLOCKS, POS], F32, bufs=3)
+            result = work.tile([P, OUT_BLOCKS, POS], F32, bufs=4)
             result_of[b] = result
 
         def add_x(b, a):
@@ -311,10 +341,12 @@ def tile_nonlocalblock_pa_t_kernel(
         def quantise_y(b):
             y_of[b] = quantise("y", y_bf_of[b][:].rearrange("p i t -> p (i t)"))
 
-        for n in range(AHEAD):
-            scores_block(n)
+        for chunks in (range(CHUNKS // 2), range(CHUNKS // 2, CHUNKS)):
+            for n in range(AHEAD):
+                scores_passes(n, chunks)
+        turn_pos(1, pos_high, nc.scalar.copy)
 
-        for n in range(PACK * MAPS):
+        for n in range(PACK * MAPS - 2):
             k, t = divmod(n, PACK)
             if t == 0:
                 if k + 2 < MAPS:
@@ -329,104 +361,113 @@ def tile_nonlocalblock_pa_t_kernel(
             if n > 0:
                 exponentials(*divmod(n - 1, PACK))
             for r in range(POS // P):
-                b = due(n, 10 + r)
+                b = due(n, 9 + r)
                 if b >= 0:
                     unload_y(b, r)
-            b = due(n, 15)
-            if b >= 0:
-                new_result(b)
-                unload_product(b, 1)
             for block, offset in enumerate((3, 4, 5, 5)):
                 b = due(n, offset)
                 if b >= 0:
                     scale_rows(b, block)
                     if block == PACK - 1:
-                        regroup(b, nc.gpsimd)
+                        regroup(b)
             add_pos(k, t)
-            b = due(n, 9)
+            b = due(n, 5)
             if b >= 0:
-                quantise_attn(b)
+                add_decoder(b, 0)
             b = due(n, 8)
             if b >= 0:
                 quantise_g(b)
-            for half in range(2):
-                b = due(n, 5 + half)
-                if b >= 0:
-                    add_decoder(b, half)
-            b = due(n, 14)
+                quantise_attn(b)
+            b = due(n, 13)
             if b >= 0:
                 quantise_y(b)
-            row_max(k, t)
-            b = due(n, 15)
+            b = due(n, 5)
             if b >= 0:
-                add_x(b, 0)
-                add_x_later(b, 1)
-                store(b)
+                add_decoder(b, 1)
+            for a in range(OUT_BLOCKS):
+                b = due(n, 14 + a)
+                if b >= 0:
+                    if a == 0:
+                        new_result(b)
+                    add_x(b, a)
+                    if a == OUT_BLOCKS - 1:
+                        store(b)
+            row_max(k, t)
             for first, offset in ((0, 2), (2, 4)):
                 b = due(n, offset)
                 if b >= 0:
                     invert_sums(b, first)
-            if t % 2 == 1 and n + AHEAD < PACK * MAPS:
-                scores_block(n + AHEAD)
             if n == 2:
                 for half in range(2):
                     unload_half(flip_half(dec_sb, half), dec_t, half)
-            if n == 8:
-                prepare_w()
             b = due(n, 4)
             if b >= 0:
                 for half in range(2):
                     flip_of[b, half] = flip_half(gproj_of[b], half)
+            scores_block(n + AHEAD)
+            if n == 7:
+                prepare_w()
             for r in range(POS // P):
-                b = due(n, 9 + r)
+                b = due(n, 8 + r)
                 if b >= 0:
                     mix(b, r)
-            if t % 2 == 0 and n + AHEAD < PACK * MAPS:
-                scores_block(n + AHEAD)
-            b = due(n, 14)
+            b = due(n, 13)
             if b >= 0:
                 project(b)
 
         z = MAPS - 1
+        exponentials(z, 1)
+        row_max(z, 2)
+        exponentials(z, 2)
+        row_max(z, 3)
         exponentials(z, 3)
-        mix(z - 2, 3)
+        unload_y(z - 2, 1)
         for half in range(2):
             flip_of[z, half] = flip_half(gproj_of[z], half)
-        quantise_g(z - 1)
-        quantise_attn(z - 1)
+        new_result(z - 3)
+        add_x(z - 3, 0)
+        invert_sums(z, 0)
+        scale_rows_on_gpsimd(z, 0)
+        scale_rows_on_gpsimd(z, 1)
+        add_x(z - 3, 1)
+        store(z - 3)
         invert_sums(z, 2)
-        for block in range(1, PACK):
-            scale_rows(z, block)
+        scale_rows(z, 2)
+        scale_rows(z, 3)
+        for r in range(2, POS // P):
+            mix(z - 2, r)
+            unload_y(z - 2, r)
+        quantise_g(z - 1)
         add_decoder(z, 0)
-        unload_y(z - 2, 2)
-        mix(z - 1, 0)
-        unload_y(z - 2, 3)
-        mix(z - 1, 1)
+        quantise_attn(z - 1)
         add_decoder(z, 1)
-        regroup(z, nc.vector)
+        regroup_on_vector(z)
         quantise_g(z)
+        for r in range(POS // P):
+            mix(z - 1, r)
+            unload_y(z - 1, r)
+        quantise_y(z - 2)
+        project(z - 2)
         quantise_attn(z)
         for r in range(POS // P):
-            if r >= 2:
-                mix(z - 1, r)
-            unload_y(z - 1, r)
-        for r in range(POS // P):
             mix(z, r, psum_scores, "scores")
-        quantise_y(z - 2)
-        for r in range(3):
-            unload_y(z, r)
-        project(z - 2)
-        quantise_y(z - 1)
-        unload_y(z, 3, nc.vector.tensor_copy)
         new_result(z - 2)
         add_x(z - 2, 0)
-        quantise_y(z)
-        add_x(z - 2, 1)
+        unload_product(z - 2, 1)
+        add_x_later(z - 2, 1)
         store(z - 2)
+        quantise_y(z - 1)
         project(z - 1)
+        for r in range(3):
+            unload_y(z, r)
+        unload_y(z, 3, nc.vector.tensor_copy)
+        new_result(z - 1)
+        add_x(z - 1, 0)
+        quantise_y(z)
         project(z, psum_scores, "scores")
-        for b in (z - 1, z):
-            new_result(b)
-            for a in range(OUT_BLOCKS):
-                add_x(b, a)
-                store(b, a)
+        add_x(z - 1, 1)
+        store(z - 1)
+        new_result(z)
+        for a in range(OUT_BLOCKS):
+            add_x(z, a)
+            store(z, a)

@@ -162,6 +162,8 @@ def tile_nonlocalblock_pa_t_kernel(
                 out=w_grouped[:].bitcast(F32).rearrange("p (a r u) -> p a r u", a=OUT_BLOCKS, u=2),
                 in_=bank[:].rearrange("p a u r -> p a r u"),
             )
+
+        def quantise_w():
             nc.vector.quantize_mx(out=w_codes[:].bitcast(FP8X4), scales=w_scales[:], in_=w_grouped[:])
 
         def new_softmax(b):
@@ -360,8 +362,8 @@ def tile_nonlocalblock_pa_t_kernel(
                 new_softmax(k)
             if n > 0:
                 exponentials(*divmod(n - 1, PACK))
-            for r in range(POS // P):
-                b = due(n, 9 + r)
+            for r, offset in enumerate((10, 10, 12, 12)):
+                b = due(n, offset)
                 if b >= 0:
                     unload_y(b, r)
             for block, offset in enumerate((3, 4, 5, 5)):
@@ -381,6 +383,8 @@ def tile_nonlocalblock_pa_t_kernel(
             b = due(n, 13)
             if b >= 0:
                 quantise_y(b)
+            if n == 9:
+                quantise_w()
             b = due(n, 5)
             if b >= 0:
                 add_decoder(b, 1)
@@ -397,6 +401,7 @@ def tile_nonlocalblock_pa_t_kernel(
                 b = due(n, offset)
                 if b >= 0:
                     invert_sums(b, first)
+            scores_block(n + AHEAD)
             if n == 2:
                 for half in range(2):
                     unload_half(flip_half(dec_sb, half), dec_t, half)
@@ -404,11 +409,10 @@ def tile_nonlocalblock_pa_t_kernel(
             if b >= 0:
                 for half in range(2):
                     flip_of[b, half] = flip_half(gproj_of[b], half)
-            scores_block(n + AHEAD)
             if n == 7:
                 prepare_w()
-            for r in range(POS // P):
-                b = due(n, 8 + r)
+            for r, offset in enumerate((9, 9, 11, 11)):
+                b = due(n, offset)
                 if b >= 0:
                     mix(b, r)
             b = due(n, 13)
@@ -421,7 +425,8 @@ def tile_nonlocalblock_pa_t_kernel(
         exponentials(z, 2)
         row_max(z, 3)
         exponentials(z, 3)
-        unload_y(z - 2, 1)
+        for r in range(2):
+            unload_y(z - 2, r)
         for half in range(2):
             flip_of[z, half] = flip_half(gproj_of[z], half)
         new_result(z - 3)

@@ -20,6 +20,7 @@ P = 128
 PACK = 4
 CHUNKS = CH // P
 OUT_BLOCKS = OUT_CH // P
+WARM_UP = 5
 AHEAD = 2
 
 FLOPS = 2 * MAPS * (2 * POS * POS * CH + OUT_CH * CH * POS)
@@ -42,6 +43,12 @@ def tile_nonlocalblock_pa_t_kernel(
         make_identity(nc, ident_bf[:])
 
         ctx.enter_context(tc.manual_schedule())
+
+        zeros = const.tile([P, POS], BF16)
+        nc.vector.memset(zeros[:], 0.0)
+        unread = psum_rest.tile([P, POS], F32, tag="rest")
+        for i in range(WARM_UP):
+            nc.tensor.matmul(out=unread[:], lhsT=zeros[:, :P], rhs=zeros[:], start=True, stop=True)
 
         theta_of, phi_of, gproj_of, x_of = {}, {}, {}, {}
         scores_of = {}
@@ -225,13 +232,15 @@ def tile_nonlocalblock_pa_t_kernel(
                 op1=ALU.add,
             )
 
-        def regroup(b):
+        def new_attn(b):
             attn_bf = work.tile([P, POS, PACK], BF16, align_bytes=64)
             attn_bf_of[b] = attn_bf
-            for r in range(POS // P):
+
+        def regroup(b, parts=range(POS // P)):
+            for r in parts:
                 cols = slice(r * P, (r + 1) * P)
                 nc.gpsimd.tensor_scalar(
-                    out=attn_bf[:, cols, :],
+                    out=attn_bf_of[b][:, cols, :],
                     in0=rows_of[b][:, :, cols].rearrange("p t i -> p i t"),
                     scalar1=1.0,
                     scalar2=0.0,
@@ -239,12 +248,10 @@ def tile_nonlocalblock_pa_t_kernel(
                     op1=ALU.add,
                 )
 
-        def regroup_on_vector(b):
-            attn_bf = work.tile([P, POS, PACK], BF16, align_bytes=64)
-            attn_bf_of[b] = attn_bf
+        def regroup_on_vector(b, cols):
             nc.vector.tensor_copy(
-                out=attn_bf[:].rearrange("p (c i) t -> p c t i", i=4),
-                in_=rows_of[b][:].rearrange("p t (c i) -> p c t i", i=4),
+                out=attn_bf_of[b][:, cols, :].rearrange("p (c i) t -> p c t i", i=4),
+                in_=rows_of[b][:, :, cols].rearrange("p t (c i) -> p c t i", i=4),
             )
 
         def quantise(what, grouped):
@@ -360,7 +367,7 @@ def tile_nonlocalblock_pa_t_kernel(
                 if k == MAPS - 1:
                     load_x(k)
                 new_softmax(k)
-            if n > 0:
+            if n > 0 and t != 1:
                 exponentials(*divmod(n - 1, PACK))
             for r, offset in enumerate((10, 10, 12, 12)):
                 b = due(n, offset)
@@ -371,7 +378,10 @@ def tile_nonlocalblock_pa_t_kernel(
                 if b >= 0:
                     scale_rows(b, block)
                     if block == PACK - 1:
+                        new_attn(b)
                         regroup(b)
+            if t == 1:
+                exponentials(k, 0)
             add_pos(k, t)
             b = due(n, 5)
             if b >= 0:
@@ -439,6 +449,8 @@ def tile_nonlocalblock_pa_t_kernel(
         invert_sums(z, 2)
         scale_rows(z, 2)
         scale_rows(z, 3)
+        new_attn(z)
+        regroup(z, range(POS // P // 2, POS // P))
         for r in range(2, POS // P):
             mix(z - 2, r)
             unload_y(z - 2, r)
@@ -446,7 +458,7 @@ def tile_nonlocalblock_pa_t_kernel(
         add_decoder(z, 0)
         quantise_attn(z - 1)
         add_decoder(z, 1)
-        regroup_on_vector(z)
+        regroup_on_vector(z, slice(0, POS // 2))
         quantise_g(z)
         for r in range(POS // P):
             mix(z - 1, r)

from contextlib import ExitStack

import concourse.mybir as mybir
from concourse.masks import make_identity

F32 = mybir.dt.float32
BF16 = mybir.dt.bfloat16
U32 = mybir.dt.uint32
U8 = mybir.dt.uint8
FP8X4 = mybir.dt.float8_e4m3fn_x4
ALU = mybir.AluOpType
ACT = mybir.ActivationFunctionType
AXIS = mybir.AxisListType

MAPS = 16
CH = 512
POS = 512
OUT_CH = 256
P = 128
PACK = 4
CHUNKS = CH // P
OUT_BLOCKS = OUT_CH // P
WARM_UP = 5
AHEAD = 2

FLOPS = 2 * MAPS * (2 * POS * POS * CH + OUT_CH * CH * POS)


def tile_nonlocalblock_pa_t_kernel(
    tc, theta, phi, g_proj, pos_embedding, pos_embedding_decoder, w_mask, x, out
):
    nc = tc.nc
    with ExitStack() as ctx:
        const = ctx.enter_context(tc.tile_pool(name="const", bufs=1))
        loads = ctx.enter_context(tc.tile_pool(name="loads", bufs=3))
        work = ctx.enter_context(tc.tile_pool(name="work", bufs=2))
        psum_scores = ctx.enter_context(tc.psum_pool(name="psum_scores", bufs=4))
        psum_rest = ctx.enter_context(tc.psum_pool(name="psum_rest", bufs=4))

        ident = const.tile([P, P], F32)
        make_identity(nc, ident[:])
        ident_bf = const.tile([P, P], BF16)
        make_identity(nc, ident_bf[:])

        ctx.enter_context(tc.manual_schedule())

        zeros = const.tile([P, POS], BF16)
        nc.vector.memset(zeros[:], 0.0)
        unread = psum_rest.tile([P, POS], F32, tag="rest")
        for i in range(WARM_UP):
            nc.tensor.matmul(out=unread[:], lhsT=zeros[:, :P], rhs=zeros[:], start=True, stop=True)

        theta_of, phi_of, gproj_of, x_of = {}, {}, {}, {}
        scores_of = {}
        soft_of, rows_of, attn_bf_of, g_bf_of, y_bf_of, result_of = {}, {}, {}, {}, {}, {}
        g_of, attn_of, y_of = {}, {}, {}
        flip_of, bank_of = {}, {}

        def load_scores_operands(b, parts=1):
            phi_sb = loads.tile([P, CHUNKS, 2, P, 2], BF16)
            theta_sb = loads.tile([P, CHUNKS, POS], BF16)
            step = CHUNKS // parts
            for first in range(0, CHUNKS, step):
                chunks = slice(first, first + step)
                nc.sync.dma_start(
                    out=phi_sb[:, chunks].rearrange("p k u q e -> p k (u q e)"),
                    in_=phi[b].rearrange("(p k) n -> p k n", k=CHUNKS)[:, chunks, :],
                )
                nc.sync.dma_start(
                    out=theta_sb[:, chunks, :], in_=theta[b].rearrange("(p k) n -> p k n", k=CHUNKS)[:, chunks, :]
                )
            phi_of[b], theta_of[b] = phi_sb, theta_sb

        def load_g(b):
            gproj_sb = loads.tile([P, CHUNKS * POS], BF16)
            nc.sync.dma_start(out=gproj_sb[:], in_=g_proj[b].rearrange("(p k) n -> p (k n)", k=CHUNKS))
            gproj_of[b] = gproj_sb

        def load_x(b):
            x_sb = loads.tile([P, OUT_BLOCKS, POS], BF16, bufs=5)
            nc.sync.dma_start(out=x_sb[:], in_=x[b].rearrange("(p a) h w -> p a (h w)", a=OUT_BLOCKS))
            x_of[b] = x_sb

        def flip_half(src, half):
            words = src[:].bitcast(F32)
            bank = psum_rest.tile([P, 2, 2, P], F32, tag="rest")
            for h in range(2):
                for u in range(2):
                    first = (2 * half + h) * (POS // 2) + u * P
                    nc.tensor.transpose(bank[:, u, h, :], words[:, first : first + P], ident[:])
            return bank

        def unload_half(bank, dst, half):
            half_words = CH * PACK // 4
            dst_words = dst[:].bitcast(F32)[:, half * half_words : (half + 1) * half_words]
            nc.scalar.copy(
                out=dst_words.rearrange("p (c u) -> p c u", u=2), in_=bank[:].rearrange("p u h c -> p (h c) u")
            )

        pos_rows = pos_embedding[0].rearrange("(a p) j -> p a j", p=P)
        pos_low = const.tile([P, PACK, POS // 2], BF16)
        pos_high = const.tile([P, PACK, POS // 2], BF16)
        nc.sync.dma_start(out=pos_low[:], in_=pos_rows[:, :, : POS // 2])
        load_scores_operands(0, parts=2)
        nc.sync.dma_start(out=pos_high[:], in_=pos_rows[:, :, POS // 2 :])
        load_scores_operands(1)
        dec_sb = const.tile([P, CHUNKS * POS], BF16)
        nc.sync.dma_start(
            out=dec_sb[:], in_=pos_embedding_decoder[0].rearrange("(p k) h w -> p (k h w)", k=CHUNKS)
        )
        load_g(0)
        w_sb = const.tile([P, OUT_BLOCKS * CH], BF16)
        nc.sync.dma_start(out=w_sb[:], in_=w_mask.rearrange("(p a) c -> p (a c)", a=OUT_BLOCKS))

        pos_t = const.tile([P, PACK, POS], BF16)

        def turn_pos(u, half, copy):
            pos_words = half[:].rearrange("p a j -> p (a j)").bitcast(F32)
            bank = psum_rest.tile([P, PACK, P], F32, tag="rest")
            for a in range(PACK):
                nc.tensor.transpose(bank[:, a, :], pos_words[:, a * P : (a + 1) * P], ident[:])
            pairs = bank[:].rearrange("p a i -> p (a i)").bitcast(BF16)
            copy(out=pos_t[:, 2 * u : 2 * u + 2, :], in_=pairs.rearrange("p (i e) -> p e i", e=2))

        turn_pos(0, pos_low, nc.vector.tensor_copy)

        def pos_on_tensor(b, t):
            if b == 0:
                return False
            return b == MAPS - 1 or t % 2 == 1

        def scores_passes(n, chunks):
            b, t = divmod(n, PACK)
            u, e = divmod(t, 2)
            if chunks[0] == 0:
                acc = psum_scores.tile([P, POS], F32, tag="scores")
                scores_of[n] = acc
            acc = scores_of[n]
            closed = chunks[-1] == CHUNKS - 1
            for k in chunks:
                nc.tensor.matmul(
                    out=acc[:],
                    lhsT=phi_of[b][:, k, u, :, e],
                    rhs=theta_of[b][:, k, :],
                    start=(k == 0),
                    stop=(k == CHUNKS - 1 and not pos_on_tensor(b, t)),
                )
            if closed and pos_on_tensor(b, t):
                nc.tensor.matmul(out=acc[:], lhsT=ident_bf[:], rhs=pos_t[:, t, :], start=False, stop=True)

        def scores_block(n):
            scores_passes(n, range(CHUNKS))

        dec_t = const.tile([P, CHUNKS * P * PACK], BF16)

        w_grouped = const.tile([P, OUT_CH * PACK], BF16, align_bytes=64)
        w_codes = const.tile([P, OUT_CH], U32, align_bytes=64)
        w_scales = const.tile([P, OUT_CH], U8, align_bytes=64)

        def prepare_w():
            w_words = w_sb[:].bitcast(F32)
            bank = psum_rest.tile([P, OUT_BLOCKS, 2, P], F32, tag="rest")
            for a in range(OUT_BLOCKS):
                for u in range(2):
                    nc.tensor.transpose(
                        bank[:, a, u, :], w_words[:, a * (CH // 2) + u : (a + 1) * (CH // 2) : 2], ident[:]
                    )
            nc.scalar.copy(
                out=w_grouped[:].bitcast(F32).rearrange("p (a r u) -> p a r u", a=OUT_BLOCKS, u=2),
                in_=bank[:].rearrange("p a u r -> p a r u"),
            )

        def quantise_w():
            nc.vector.quantize_mx(out=w_codes[:].bitcast(FP8X4), scales=w_scales[:], in_=w_grouped[:])

        def new_softmax(b):
            shifted = work.tile([P, PACK, POS], F32)
            expd = work.tile([P, PACK, POS], F32)
            neg_max = work.tile([P, PACK], F32)
            row_sum = work.tile([P, PACK], F32)
            inv_sum = work.tile([P, PACK], F32)
            soft_of[b] = (shifted, expd, neg_max, row_sum, inv_sum)
            attn_rows = work.tile([P, PACK, POS], BF16)
            rows_of[b] = attn_rows

        def with_pos(b, t):
            if pos_on_tensor(b, t):
                return scores_of[PACK * b + t][:]
            return soft_of[b][0][:, t, :]

        def add_pos(b, t):
            if not pos_on_tensor(b, t):
                nc.vector.tensor_tensor(
                    out=with_pos(b, t), in0=scores_of[PACK * b + t][:], in1=pos_t[:, t, :], op=ALU.add
                )

        def row_max(b, t):
            neg_max = soft_of[b][2]
            nc.vector.tensor_reduce(
                out=neg_max[:, t : t + 1], in_=with_pos(b, t), axis=AXIS.X, op=ALU.max, negate=True
            )

        def exponentials(b, t):
            expd, neg_max, row_sum = soft_of[b][1:4]
            nc.scalar.activation(
                out=expd[:, t, :],
                in_=with_pos(b, t),
                func=ACT.Exp,
                bias=neg_max[:, t : t + 1],
                scale=1.0,
                accum_out=row_sum[:, t : t + 1],
            )

        def invert_sums(b, first):
            row_sum, inv_sum = soft_of[b][3], soft_of[b][4]
            nc.vector.reciprocal(out=inv_sum[:, first : first + 2], in_=row_sum[:, first : first + 2])

        def scale_rows(b, t):
            expd, inv_sum = soft_of[b][1], soft_of[b][4]
            nc.scalar.activation(
                out=rows_of[b][:, t, :], in_=expd[:, t, :], func=ACT.Copy, scale=inv_sum[:, t : t + 1]
            )

        def scale_rows_on_gpsimd(b, t):
            expd, inv_sum = soft_of[b][1], soft_of[b][4]
            nc.gpsimd.tensor_scalar(
                out=rows_of[b][:, t, :],
                in0=expd[:, t, :],
                scalar1=inv_sum[:, t : t + 1],
                scalar2=0.0,
                op0=ALU.mult,
                op1=ALU.add,
            )

        def new_attn(b):
            attn_bf = work.tile([P, POS, PACK], BF16, align_bytes=64)
            attn_bf_of[b] = attn_bf

        def regroup(b, parts=range(POS // P)):
            for r in parts:
                cols = slice(r * P, (r + 1) * P)
                nc.gpsimd.tensor_scalar(
                    out=attn_bf_of[b][:, cols, :],
                    in0=rows_of[b][:, :, cols].rearrange("p t i -> p i t"),
                    scalar1=1.0,
                    scalar2=0.0,
                    op0=ALU.mult,
                    op1=ALU.add,
                )

        def regroup_on_vector(b, cols):
            nc.vector.tensor_copy(
                out=attn_bf_of[b][:, cols, :].rearrange("p (c i) t -> p c t i", i=4),
                in_=rows_of[b][:, :, cols].rearrange("p t (c i) -> p c t i", i=4),
            )

        def quantise(what, grouped):
            codes = work.tile([P, POS], U32, align_bytes=64, name=what + "_codes", tag=what + "_codes")
            scales = work.tile([P, POS], U8, align_bytes=64, name=what + "_scales", tag=what + "_scales")
            nc.vector.quantize_mx(out=codes[:].bitcast(FP8X4), scales=scales[:], in_=grouped)
            return codes, scales

        def add_decoder(b, half):
            if half == 0:
                g_bf = work.tile([P, CH * PACK], BF16, align_bytes=64)
                g_bf_of[b] = g_bf
            g_bf, bank = g_bf_of[b], flip_of[b, half]
            cols = slice(half * CH * PACK // 2, (half + 1) * CH * PACK // 2)
            pairs = bank[:].rearrange("p u h c -> p (u h c)").bitcast(BF16)
            nc.vector.tensor_tensor(
                out=g_bf[:, cols].rearrange("p (c u e) -> p c u e", u=2, e=2),
                in0=pairs.rearrange("p (u c e) -> p c u e", u=2, e=2),
                in1=dec_t[:, cols].rearrange("p (c u e) -> p c u e", u=2, e=2),
                op=ALU.add,
            )

        def mix(b, r, pool=psum_rest, tag="rest"):
            g_codes, g_scales = g_of[b]
            a_codes, a_scales = attn_of[b]
            cols = slice(r * P, (r + 1) * P)
            bank = pool.tile([P, PACK, P], F32, tag=tag)
            for t in range(PACK):
                group = slice(t * P, (t + 1) * P)
                nc.tensor.matmul_mx(
                    out=bank[:, t, :],
                    lhsT=g_codes[:, group].bitcast(FP8X4),
                    lhsT_scale=g_scales[:, group],
                    rhs=a_codes[:, cols].bitcast(FP8X4),
                    rhs_scale=a_scales[:, cols],
                    start=True,
                    stop=True,
                )
            bank_of["y", b, r] = bank

        def unload_y(b, r, copy=nc.scalar.copy):
            if r == 0:
                y_bf = work.tile([P, POS, PACK], BF16, align_bytes=64)
                y_bf_of[b] = y_bf
            cols = slice(r * P, (r + 1) * P)
            copy(out=y_bf_of[b][:, cols, :], in_=bank_of["y", b, r][:].rearrange("p t i -> p i t"))

        def project(b, pool=psum_rest, tag="rest"):
            y_codes, y_scales = y_of[b]
            for a in range(OUT_BLOCKS):
                rows = slice(a * P, (a + 1) * P)
                bank = pool.tile([P, POS], F32, tag=tag)
                nc.tensor.matmul_mx(
                    out=bank[:],
                    lhsT=w_codes[:, rows].bitcast(FP8X4),
                    lhsT_scale=w_scales[:, rows],
                    rhs=y_codes[:].bitcast(FP8X4),
                    rhs_scale=y_scales[:],
                    start=True,
                    stop=True,
                )
                bank_of["out", b, a] = bank

        def new_result(b):
            result = work.tile([P, OUT_BLOCKS, POS], F32, bufs=4)
            result_of[b] = result

        def add_x(b, a):
            nc.vector.tensor_tensor(
                out=result_of[b][:, a, :], in0=bank_of["out", b, a][:], in1=x_of[b][:, a, :], op=ALU.add
            )

        def unload_product(b, a):
            nc.scalar.copy(out=result_of[b][:, a, :], in_=bank_of["out", b, a][:])

        def add_x_later(b, a):
            for half in range(2):
                cols = slice(half * POS // 2, (half + 1) * POS // 2)
                product = result_of[b][:, a, cols]
                nc.gpsimd.tensor_tensor(out=product, in0=product, in1=x_of[b][:, a, cols], op=ALU.add)

        def store(b, a=slice(0, OUT_BLOCKS)):
            rows = out[b].rearrange("(p a) h w -> p a (h w)", a=OUT_BLOCKS)
            nc.sync.dma_start(out=rows[:, a, :], in_=result_of[b][:, a, :])

        def due(n, offset):
            b, rest = divmod(n - offset, PACK)
            return b if rest == 0 and 0 <= b < MAPS else -1

        def quantise_attn(b):
            attn_of[b] = quantise("attn", attn_bf_of[b][:].rearrange("p i t -> p (i t)"))

        def quantise_g(b):
            g_of[b] = quantise("g", g_bf_of[b][:])

        def quantise_y(b):
            y_of[b] = quantise("y", y_bf_of[b][:].rearrange("p i t -> p (i t)"))

        for chunks in (range(CHUNKS // 2), range(CHUNKS // 2, CHUNKS)):
            for n in range(AHEAD):
                scores_passes(n, chunks)
        turn_pos(1, pos_high, nc.scalar.copy)

        for n in range(PACK * MAPS - 2):
            k, t = divmod(n, PACK)
            if t == 0:
                if k + 2 < MAPS:
                    load_scores_operands(k + 2)
                if k + 1 < MAPS:
                    load_g(k + 1)
                if k >= 1:
                    load_x(k - 1)
                if k == MAPS - 1:
                    load_x(k)
                new_softmax(k)
            if n > 0 and t != 1:
                exponentials(*divmod(n - 1, PACK))
            for r, offset in enumerate((10, 10, 12, 12)):
                b = due(n, offset)
                if b >= 0:
                    unload_y(b, r)
            for block, offset in enumerate((3, 4, 5, 5)):
                b = due(n, offset)
                if b >= 0:
                    scale_rows(b, block)
                    if block == PACK - 1:
                        new_attn(b)
                        regroup(b)
            if t == 1:
                exponentials(k, 0)
            add_pos(k, t)
            b = due(n, 5)
            if b >= 0:
                add_decoder(b, 0)
            b = due(n, 8)
            if b >= 0:
                quantise_g(b)
                quantise_attn(b)
            b = due(n, 13)
            if b >= 0:
                quantise_y(b)
            if n == 9:
                quantise_w()
            b = due(n, 5)
            if b >= 0:
                add_decoder(b, 1)
            for a in range(OUT_BLOCKS):
                b = due(n, 14 + a)
                if b >= 0:
                    if a == 0:
                        new_result(b)
                    add_x(b, a)
                    if a == OUT_BLOCKS - 1:
                        store(b)
            row_max(k, t)
            for first, offset in ((0, 2), (2, 4)):
                b = due(n, offset)
                if b >= 0:
                    invert_sums(b, first)
            scores_block(n + AHEAD)
            if n == 2:
                for half in range(2):
                    unload_half(flip_half(dec_sb, half), dec_t, half)
            b = due(n, 4)
            if b >= 0:
                for half in range(2):
                    flip_of[b, half] = flip_half(gproj_of[b], half)
            if n == 7:
                prepare_w()
            for r, offset in enumerate((9, 9, 11, 11)):
                b = due(n, offset)
                if b >= 0:
                    mix(b, r)
            b = due(n, 13)
            if b >= 0:
                project(b)

        z = MAPS - 1
        exponentials(z, 1)
        row_max(z, 2)
        exponentials(z, 2)
        row_max(z, 3)
        exponentials(z, 3)
        for r in range(2):
            unload_y(z - 2, r)
        for half in range(2):
            flip_of[z, half] = flip_half(gproj_of[z], half)
        new_result(z - 3)
        add_x(z - 3, 0)
        invert_sums(z, 0)
        scale_rows_on_gpsimd(z, 0)
        scale_rows_on_gpsimd(z, 1)
        add_x(z - 3, 1)
        store(z - 3)
        invert_sums(z, 2)
        scale_rows(z, 2)
        scale_rows(z, 3)
        new_attn(z)
        regroup(z, range(POS // P // 2, POS // P))
        for r in range(2, POS // P):
            mix(z - 2, r)
            unload_y(z - 2, r)
        quantise_g(z - 1)
        add_decoder(z, 0)
        quantise_attn(z - 1)
        add_decoder(z, 1)
        regroup_on_vector(z, slice(0, POS // 2))
        quantise_g(z)
        for r in range(POS // P):
            mix(z - 1, r)
            unload_y(z - 1, r)
        quantise_y(z - 2)
        project(z - 2)
        quantise_attn(z)
        for r in range(POS // P):
            mix(z, r, psum_scores, "scores")
        new_result(z - 2)
        add_x(z - 2, 0)
        unload_product(z - 2, 1)
        add_x_later(z - 2, 1)
        store(z - 2)
        quantise_y(z - 1)
        project(z - 1)
        for r in range(3):
            unload_y(z, r)
        unload_y(z, 3, nc.vector.tensor_copy)
        new_result(z - 1)
        add_x(z - 1, 0)
        quantise_y(z)
        project(z, psum_scores, "scores")
        add_x(z - 1, 1)
        store(z - 1)
        new_result(z)
        for a in range(OUT_BLOCKS):
            add_x(z, a)
            store(z, a)
